import numpy as np
import ml_dtypes


def mxq(x, axis, fmt="e4m3"):
    dtype, down = {"e4m3": (ml_dtypes.float8_e4m3fn, 7), "e5m2": (ml_dtypes.float8_e5m2, 14)}[fmt]
    v = np.moveaxis(np.asarray(x, np.float32).astype(ml_dtypes.bfloat16).astype(np.float64), axis, -1)
    blocks = v.reshape(v.shape[:-1] + (-1, 32))
    amax = np.abs(blocks).max(-1, keepdims=True)
    byte = np.maximum(np.where(amax > 0, np.frexp(amax)[1] - 1 + 127, 0) - down, 1)
    scale = np.exp2(byte - 127.0)
    codes = (blocks / scale).astype(np.float32).astype(dtype).astype(np.float64)
    return np.moveaxis((codes * scale).reshape(v.shape), -1, axis)


WIDE = False


def mx_kscale(k):
    if not WIDE:
        return np.ones(k)
    levels = np.array([10, -10, 5, -5, 0])
    a = np.random.permutation(np.resize(levels, k // 512 * 4)).reshape(k // 512, 4)
    idx = np.arange(k)
    return np.exp2(a[idx // 512, idx % 128 // 32])


BF16 = ml_dtypes.bfloat16


def bf(x):
    return np.asarray(x, np.float32).astype(BF16)


def f64(x):
    return np.asarray(x).astype(np.float64)


B, F, A, U = 512, 128, 8, 32
R = 2.0
KLIM = 1.0
XLIM = 1.5
ROWSUM = -4.0


def softmax(v):
    e = np.exp(v - v.max(-1, keepdims=True))
    return e / e.sum(-1, keepdims=True)


def setup_inputs():
    s = mx_kscale(F * U).reshape(F, U)[:, 0]
    d = np.log2(s / s.min())
    sign = np.where(np.arange(U) < U // 2, 1.0, -1.0)
    c = np.log(2.0) / R * d[:, None] * sign[None, :]
    g = np.log(F / np.sum(2.0 ** -d)) / R
    x = np.clip(np.random.standard_normal((B, F)) * 5.0 / np.sqrt(F), -XLIM, XLIM)
    x = x - x.mean(1, keepdims=True) + ROWSUM / F
    xm = (1.0 - np.eye(F))[:, None, :] * x[None, :, :]
    k = np.random.uniform(-KLIM, KLIM, (F, A, F, U)) + c[:, None, None, :] + g
    return {"xm": bf(xm), "kernels": bf(k)}


def reference(xm, kernels):
    xm, k = f64(xm), f64(kernels)
    logits = (xm @ k.transpose(0, 2, 1, 3).reshape(F, F, A * U)).reshape(F, B, A, U)
    z = softmax(logits)
    w = np.exp(k * R)
    zc = z.transpose(2, 1, 0, 3).reshape(A, B, F * U)
    wc = w.transpose(1, 0, 3, 2).reshape(A, F * U, F)
    scores = (mxq(zc, 2, "e4m3") @ mxq(wc, 1, "e4m3")) / F
    return softmax(scores)

@@ -1,0 +1,219 @@
+from contextlib import ExitStack
+
+import concourse.mybir as mybir
+from concourse.masks import make_identity
+
+BF16 = mybir.dt.bfloat16
+F32 = mybir.dt.float32
+U32 = mybir.dt.uint32
+U8 = mybir.dt.uint8
+FP8X4 = mybir.dt.float8_e4m3fn_x4
+ALU = mybir.AluOpType
+ACT = mybir.ActivationFunctionType
+AXIS = mybir.AxisListType
+
+P = 128
+J = 128
+B = 512
+F = 128
+A = 8
+U = 32
+PACK = 4
+UH = U // PACK
+J_PASS = P // UH
+N_PASS = J // J_PASS
+ROW_TILES = B // P
+J_QUARTER = 4
+J_BANK = 2
+
+FLOPS = 2 * J * B * F * A * U + 2 * A * B * J * U * F
+
+
+def tile_iterativefeatureexclusion_pa_kernel(tc, xm, kernels, out):
+    nc = tc.nc
+    with ExitStack() as ctx:
+        const = ctx.enter_context(tc.tile_pool(name="const", bufs=1))
+        keep = ctx.enter_context(tc.tile_pool(name="keep", bufs=1))
+        loads = ctx.enter_context(tc.tile_pool(name="loads", bufs=2))
+        work = ctx.enter_context(tc.tile_pool(name="work", bufs=2))
+        small = ctx.enter_context(tc.tile_pool(name="small", bufs=4))
+        psum_logits = ctx.enter_context(tc.psum_pool(name="psum_logits", bufs=3))
+        psum_xt = ctx.enter_context(tc.psum_pool(name="psum_xt", bufs=1))
+        psum_tr = ctx.enter_context(tc.psum_pool(name="psum_tr", bufs=2))
+        psum_scores = ctx.enter_context(tc.psum_pool(name="psum_scores", bufs=1))
+
+        ident_bf = const.tile([P, P], BF16)
+        make_identity(nc, ident_bf[:])
+        ident_f32 = const.tile([P, P], F32)
+        make_identity(nc, ident_f32[:])
+
+        k_sb = [keep.tile([P, A, J_PASS, U], BF16, name="k_sb%d" % c) for c in range(N_PASS)]
+        w_codes = [keep.tile([P, A * F], U32, name="w_codes%d" % c, align_bytes=64) for c in range(N_PASS)]
+        w_scales = [keep.tile([P, A * F], U8, name="w_scales%d" % c, align_bytes=64) for c in range(N_PASS)]
+        z_codes = [keep.tile([P, A * P], U32, name="z_codes%d" % c, align_bytes=64) for c in range(N_PASS)]
+        z_scales = [keep.tile([P, A * P], U8, name="z_scales%d" % c, align_bytes=64) for c in range(N_PASS)]
+
+        def load_kernels(c):
+            for a in range(A):
+                nc.sync.dma_start(
+                    out=k_sb[c][:, a, :, :],
+                    in_=kernels[c * J_PASS : (c + 1) * J_PASS, a, :, :].rearrange("j f u -> f j u"),
+                )
+
+        def load_xm(rt, c):
+            x_sb = loads.tile([P, J_PASS, F], BF16)
+            nc.sync.dma_start(
+                out=x_sb[:],
+                in_=xm[c * J_PASS : (c + 1) * J_PASS, rt * P : (rt + 1) * P, :].rearrange("j b f -> b j f"),
+            )
+            return x_sb
+
+        def quantise_weights(c):
+            grouped = work.tile([P, A, F, PACK], BF16, tag="grouped", align_bytes=64)
+            for pair in range(A // 2):
+                wt = psum_tr.tile([P, 2, 2, F], F32, tag="tr")
+                for ai in range(2):
+                    words = k_sb[c][:, 2 * pair + ai, :, :].rearrange("p j u -> p (j u)").bitcast(F32)
+                    for h in range(2):
+                        nc.tensor.transpose(
+                            wt[:, ai, h, :],
+                            words.rearrange("p (w h) -> p w h", h=2)[:, :, h],
+                            ident_f32[:],
+                        )
+                for ai in range(2):
+                    nc.scalar.activation(
+                        out=grouped[:, 2 * pair + ai, :, :].rearrange("p f (h e) -> p f h e", e=2),
+                        in_=wt[:, ai, :, :].bitcast(BF16).rearrange("p h (f e) -> p f h e", e=2),
+                        func=ACT.Exp,
+                        scale=2.0,
+                    )
+            nc.vector.quantize_mx(
+                out=w_codes[c][:].bitcast(FP8X4),
+                scales=w_scales[c][:],
+                in_=grouped[:].rearrange("p a f t -> p (a f t)"),
+            )
+
+        def exp_of_shifted_logits(x_sb, c):
+            e_sb = work.tile([P, A, PACK, J_PASS, UH], F32, tag="e_sb")
+            for q in range(J_PASS // J_QUARTER):
+                xt_ps = psum_xt.tile([P, J_QUARTER, P], BF16)
+                for i in range(J_QUARTER):
+                    nc.tensor.transpose(xt_ps[:, i, :], x_sb[:, q * J_QUARTER + i, :], ident_bf[:])
+                xt_sb = loads.tile([P, J_QUARTER, P], BF16, bufs=3)
+                nc.scalar.copy(out=xt_sb[:], in_=xt_ps[:])
+                for half in range(J_QUARTER // J_BANK):
+                    logits = psum_logits.tile([P, J_BANK, A, U], F32)
+                    jl0 = q * J_QUARTER + half * J_BANK
+                    for i in range(J_BANK):
+                        nc.tensor.matmul(
+                            out=logits[:, i, :, :],
+                            lhsT=xt_sb[:, half * J_BANK + i, :],
+                            rhs=k_sb[c][:, :, jl0 + i, :],
+                            start=True,
+                            stop=True,
+                        )
+                    top = small.tile([P, J_BANK, A], F32)
+                    nc.vector.tensor_reduce(out=top[:], in_=logits[:], axis=AXIS.X, op=ALU.max)
+                    nc.vector.tensor_tensor(
+                        out=e_sb[:, :, :, jl0 : jl0 + J_BANK, :].rearrange("p a t j h -> p j a t h"),
+                        in0=logits[:].rearrange("p j a (h t) -> p j a t h", t=PACK),
+                        in1=top[:].unsqueeze(3).unsqueeze(4).to_broadcast([P, J_BANK, A, PACK, UH]),
+                        op=ALU.subtract,
+                    )
+                quarter = e_sb[:, :, :, q * J_QUARTER : (q + 1) * J_QUARTER, :]
+                nc.scalar.activation(out=quarter, in_=quarter, func=ACT.Exp)
+            return e_sb
+
+        def normalise(e_sb):
+            total = small.tile([P, A, J_PASS], F32)
+            nc.vector.tensor_reduce(
+                out=total[:], in_=e_sb[:].rearrange("p a t j h -> p a j t h"), axis=AXIS.XY, op=ALU.add
+            )
+            inverse = small.tile([P, A, J_PASS], F32)
+            nc.vector.reciprocal(out=inverse[:], in_=total[:])
+            z_sb = work.tile([P, A, PACK, J_PASS, UH], BF16, tag="z_sb")
+            for a in range(A):
+                nc.gpsimd.tensor_tensor(
+                    out=z_sb[:, a, :, :, :],
+                    in0=e_sb[:, a, :, :, :],
+                    in1=inverse[:, a, :].unsqueeze(1).unsqueeze(3).to_broadcast([P, PACK, J_PASS, UH]),
+                    op=ALU.mult,
+                )
+            return z_sb
+
+        def quantise_z(z_sb, c):
+            grouped = work.tile([P, A, P, PACK], BF16, tag="grouped", align_bytes=64)
+            for pair in range(A // 2):
+                zt = psum_tr.tile([P, 2, PACK, P], BF16, tag="tr")
+                for ai in range(2):
+                    for t in range(PACK):
+                        nc.tensor.transpose(
+                            zt[:, ai, t, :],
+                            z_sb[:, 2 * pair + ai, t, :, :].rearrange("p j h -> p (j h)"),
+                            ident_bf[:],
+                        )
+                nc.scalar.copy(
+                    out=grouped[:, 2 * pair : 2 * pair + 2, :, :],
+                    in_=zt[:].rearrange("p a t b -> p a b t"),
+                )
+            nc.vector.quantize_mx(
+                out=z_codes[c][:].bitcast(FP8X4),
+                scales=z_scales[c][:],
+                in_=grouped[:].rearrange("p a b t -> p (a b t)"),
+            )
+
+        def finish_rows(rt):
+            banks = [psum_scores.tile([P, A // 2, F], F32, name="scores%d" % half) for half in range(2)]
+            for a in range(A):
+                cols = slice(a * P, (a + 1) * P)
+                for c in range(N_PASS):
+                    nc.tensor.matmul_mx(
+                        out=banks[a // 4][:, a % 4, :],
+                        lhsT=z_codes[c][:, cols].bitcast(FP8X4),
+                        lhsT_scale=z_scales[c][:, cols],
+                        rhs=w_codes[c][:, cols].bitcast(FP8X4),
+                        rhs_scale=w_scales[c][:, cols],
+                        start=(c == 0),
+                        stop=(c == N_PASS - 1),
+                    )
+            top = small.tile([P, A], F32, tag="score_top")
+            for half in range(2):
+                nc.vector.tensor_reduce(
+                    out=top[:, half * 4 : half * 4 + 4], in_=banks[half][:], axis=AXIS.X, op=ALU.max
+                )
+            shift = small.tile([P, A], F32, tag="score_shift")
+            nc.vector.tensor_scalar(out=shift[:], in0=top[:], scalar1=-1.0 / J, scalar2=None, op0=ALU.mult)
+            prob = work.tile([P, A, F], F32, tag="prob", bufs=1)
+            total = small.tile([P, A], F32, tag="score_total")
+            for a in range(A):
+                nc.scalar.activation(
+                    out=prob[:, a, :],
+                    in_=banks[a // 4][:, a % 4, :],
+                    func=ACT.Exp,
+                    bias=shift[:, a : a + 1],
+                    scale=1.0 / J,
+                    accum_out=total[:, a : a + 1],
+                )
+            inverse = small.tile([P, A], F32, tag="score_inverse")
+            nc.vector.reciprocal(out=inverse[:], in_=total[:])
+            nc.vector.tensor_tensor(
+                out=prob[:], in0=prob[:], in1=inverse[:].unsqueeze(2).to_broadcast([P, A, F]), op=ALU.mult
+            )
+            nc.sync.dma_start(out=out[:, rt * P : (rt + 1) * P, :].rearrange("a b f -> b a f"), in_=prob[:])
+
+        waiting = None
+        for rt in range(ROW_TILES):
+            for c in range(N_PASS):
+                if rt == 0:
+                    load_kernels(c)
+                x_sb = load_xm(rt, c)
+                e_sb = exp_of_shifted_logits(x_sb, c)
+                if rt == 0:
+                    quantise_weights(c)
+                if waiting is not None:
+                    quantise_z(waiting[0], waiting[1])
+                    if waiting[1] == N_PASS - 1:
+                        finish_rows(waiting[2])
+                waiting = (normalise(e_sb), c, rt)
+        quantise_z(waiting[0], waiting[1])
+        finish_rows(waiting[2])

@@ -23,8 +23,10 @@ UH = U // PACK
 J_PASS = P // UH
 N_PASS = J // J_PASS
 ROW_TILES = B // P
+J_STEP = J_PASS // 2
 J_QUARTER = 4
 J_BANK = 2
+N_STEPS = ROW_TILES * J // J_STEP
 
 FLOPS = 2 * J * B * F * A * U + 2 * A * B * J * U * F
 
@@ -34,12 +36,11 @@ def tile_iterativefeatureexclusion_pa_kernel(tc, xm, kernels, out):
     with ExitStack() as ctx:
         const = ctx.enter_context(tc.tile_pool(name="const", bufs=1))
         keep = ctx.enter_context(tc.tile_pool(name="keep", bufs=1))
-        loads = ctx.enter_context(tc.tile_pool(name="loads", bufs=2))
+        loads = ctx.enter_context(tc.tile_pool(name="loads", bufs=3))
         work = ctx.enter_context(tc.tile_pool(name="work", bufs=2))
         small = ctx.enter_context(tc.tile_pool(name="small", bufs=4))
-        psum_logits = ctx.enter_context(tc.psum_pool(name="psum_logits", bufs=3))
-        psum_xt = ctx.enter_context(tc.psum_pool(name="psum_xt", bufs=1))
-        psum_tr = ctx.enter_context(tc.psum_pool(name="psum_tr", bufs=2))
+        psum_logits = ctx.enter_context(tc.psum_pool(name="psum_logits", bufs=4))
+        psum_tr = ctx.enter_context(tc.psum_pool(name="psum_tr", bufs=3))
         psum_scores = ctx.enter_context(tc.psum_pool(name="psum_scores", bufs=1))
 
         ident_bf = const.tile([P, P], BF16)
@@ -53,20 +54,103 @@ def tile_iterativefeatureexclusion_pa_kernel(tc, xm, kernels, out):
         z_codes = [keep.tile([P, A * P], U32, name="z_codes%d" % c, align_bytes=64) for c in range(N_PASS)]
         z_scales = [keep.tile([P, A * P], U8, name="z_scales%d" % c, align_bytes=64) for c in range(N_PASS)]
 
-        def load_kernels(c):
-            for a in range(A):
-                nc.sync.dma_start(
-                    out=k_sb[c][:, a, :, :],
-                    in_=kernels[c * J_PASS : (c + 1) * J_PASS, a, :, :].rearrange("j f u -> f j u"),
-                )
+        def place(step):
+            return step // (2 * N_PASS), (step // 2) % N_PASS, (step % 2) * J_STEP
 
-        def load_xm(rt, c):
-            x_sb = loads.tile([P, J_PASS, F], BF16)
+        def load(step):
+            rt, c, jl0 = place(step)
+            j0 = c * J_PASS + jl0
+            if rt == 0:
+                for a in range(A):
+                    nc.sync.dma_start(
+                        out=k_sb[c][:, a, jl0 : jl0 + J_STEP, :],
+                        in_=kernels[j0 : j0 + J_STEP, a, :, :].rearrange("j f u -> f j u"),
+                    )
+            x_sb = loads.tile([P, J_STEP, F], BF16)
             nc.sync.dma_start(
-                out=x_sb[:],
-                in_=xm[c * J_PASS : (c + 1) * J_PASS, rt * P : (rt + 1) * P, :].rearrange("j b f -> b j f"),
+                out=x_sb[:], in_=xm[j0 : j0 + J_STEP, rt * P : (rt + 1) * P, :].rearrange("j b f -> b j f")
             )
             return x_sb
+
+        def transpose_xm(x_sb):
+            xt_sb = loads.tile([P, J_STEP, P], BF16)
+            for q in range(J_STEP // J_QUARTER):
+                js = slice(q * J_QUARTER, (q + 1) * J_QUARTER)
+                xt_ps = psum_tr.tile([P, J_QUARTER, P], BF16, tag="tr")
+                for i in range(J_QUARTER):
+                    nc.tensor.transpose(xt_ps[:, i, :], x_sb[:, q * J_QUARTER + i, :], ident_bf[:])
+                nc.scalar.copy(out=xt_sb[:, js, :], in_=xt_ps[:])
+            return xt_sb
+
+        def logits_and_max(step, xt_sb, q):
+            rt, c, jl0 = place(step)
+            banks = []
+            for half in range(J_QUARTER // J_BANK):
+                logits = psum_logits.tile([P, J_BANK, A, U], F32)
+                js0 = q * J_QUARTER + half * J_BANK
+                for i in range(J_BANK):
+                    nc.tensor.matmul(
+                        out=logits[:, i, :, :],
+                        lhsT=xt_sb[:, js0 + i, :],
+                        rhs=k_sb[c][:, :, jl0 + js0 + i, :],
+                        start=True,
+                        stop=True,
+                    )
+                top = small.tile([P, J_BANK, A], F32)
+                nc.vector.tensor_reduce(out=top[:], in_=logits[:], axis=AXIS.X, op=ALU.max)
+                banks.append((logits, top))
+            return banks
+
+        def exp_of_shifted_logits(banks, e_sb, q):
+            for half in range(J_QUARTER // J_BANK):
+                logits, top = banks[half]
+                js0 = q * J_QUARTER + half * J_BANK
+                nc.vector.tensor_tensor(
+                    out=e_sb[:, :, :, js0 : js0 + J_BANK, :].rearrange("p a t j h -> p j a t h"),
+                    in0=logits[:].rearrange("p j a (h t) -> p j a t h", t=PACK),
+                    in1=top[:].unsqueeze(3).unsqueeze(4).to_broadcast([P, J_BANK, A, PACK, UH]),
+                    op=ALU.subtract,
+                )
+            quarter = e_sb[:, :, :, q * J_QUARTER : (q + 1) * J_QUARTER, :]
+            nc.scalar.activation(out=quarter, in_=quarter, func=ACT.Exp)
+
+        def add_word_halves(e_sb):
+            pair_sum = work.tile([P, A, PACK // 2, J_STEP, UH], F32, tag="pair_sum")
+            nc.gpsimd.tensor_tensor(
+                out=pair_sum[:], in0=e_sb[:, :, 0 : PACK // 2, :, :], in1=e_sb[:, :, PACK // 2 : PACK, :, :], op=ALU.add
+            )
+            return pair_sum
+
+        def sum_of_units(pair_sum):
+            total = small.tile([P, A, J_STEP], F32)
+            nc.vector.tensor_reduce(
+                out=total[:], in_=pair_sum[:].rearrange("p a t j h -> p a j t h"), axis=AXIS.XY, op=ALU.add
+            )
+            return total
+
+        def normalise(step, e_sb, total, z_sb):
+            rt, c, jl0 = place(step)
+            inverse = small.tile([P, A, J_STEP], F32)
+            nc.vector.reciprocal(out=inverse[:], in_=total[:])
+            nc.gpsimd.tensor_tensor(
+                out=z_sb[:, :, :, jl0 : jl0 + J_STEP, :].rearrange("p a t j h -> p t a j h"),
+                in0=e_sb[:].rearrange("p a t j h -> p t a j h"),
+                in1=inverse[:].unsqueeze(1).unsqueeze(4).to_broadcast([P, PACK, A, J_STEP, UH]),
+                op=ALU.mult,
+            )
+
+        def transpose_z(z_sb, grouped, pair):
+            zt = psum_tr.tile([P, 2, PACK, P], BF16, tag="tr")
+            for ai in range(2):
+                for t in range(PACK):
+                    nc.tensor.transpose(
+                        zt[:, ai, t, :],
+                        z_sb[:, 2 * pair + ai, t, :, :].rearrange("p j h -> p (j h)"),
+                        ident_bf[:],
+                    )
+            nc.scalar.copy(
+                out=grouped[:, 2 * pair : 2 * pair + 2, :, :], in_=zt[:].rearrange("p a t b -> p a b t")
+            )
 
         def quantise_weights(c):
             grouped = work.tile([P, A, F, PACK], BF16, tag="grouped", align_bytes=64)
@@ -76,9 +160,7 @@ def tile_iterativefeatureexclusion_pa_kernel(tc, xm, kernels, out):
                     words = k_sb[c][:, 2 * pair + ai, :, :].rearrange("p j u -> p (j u)").bitcast(F32)
                     for h in range(2):
                         nc.tensor.transpose(
-                            wt[:, ai, h, :],
-                            words.rearrange("p (w h) -> p w h", h=2)[:, :, h],
-                            ident_f32[:],
+                            wt[:, ai, h, :], words.rearrange("p (w h) -> p w h", h=2)[:, :, h], ident_f32[:]
                         )
                 for ai in range(2):
                     nc.scalar.activation(
@@ -93,127 +175,87 @@ def tile_iterativefeatureexclusion_pa_kernel(tc, xm, kernels, out):
                 in_=grouped[:].rearrange("p a f t -> p (a f t)"),
             )
 
-        def exp_of_shifted_logits(x_sb, c):
-            e_sb = work.tile([P, A, PACK, J_PASS, UH], F32, tag="e_sb")
-            for q in range(J_PASS // J_QUARTER):
-                xt_ps = psum_xt.tile([P, J_QUARTER, P], BF16)
-                for i in range(J_QUARTER):
-                    nc.tensor.transpose(xt_ps[:, i, :], x_sb[:, q * J_QUARTER + i, :], ident_bf[:])
-                xt_sb = loads.tile([P, J_QUARTER, P], BF16, bufs=3)
-                nc.scalar.copy(out=xt_sb[:], in_=xt_ps[:])
-                for half in range(J_QUARTER // J_BANK):
-                    logits = psum_logits.tile([P, J_BANK, A, U], F32)
-                    jl0 = q * J_QUARTER + half * J_BANK
-                    for i in range(J_BANK):
-                        nc.tensor.matmul(
-                            out=logits[:, i, :, :],
-                            lhsT=xt_sb[:, half * J_BANK + i, :],
-                            rhs=k_sb[c][:, :, jl0 + i, :],
-                            start=True,
-                            stop=True,
-                        )
-                    top = small.tile([P, J_BANK, A], F32)
-                    nc.vector.tensor_reduce(out=top[:], in_=logits[:], axis=AXIS.X, op=ALU.max)
-                    nc.vector.tensor_tensor(
-                        out=e_sb[:, :, :, jl0 : jl0 + J_BANK, :].rearrange("p a t j h -> p j a t h"),
-                        in0=logits[:].rearrange("p j a (h t) -> p j a t h", t=PACK),
-                        in1=top[:].unsqueeze(3).unsqueeze(4).to_broadcast([P, J_BANK, A, PACK, UH]),
-                        op=ALU.subtract,
-                    )
-                quarter = e_sb[:, :, :, q * J_QUARTER : (q + 1) * J_QUARTER, :]
-                nc.scalar.activation(out=quarter, in_=quarter, func=ACT.Exp)
-            return e_sb
-
-        def normalise(e_sb):
-            total = small.tile([P, A, J_PASS], F32)
-            nc.vector.tensor_reduce(
-                out=total[:], in_=e_sb[:].rearrange("p a t j h -> p a j t h"), axis=AXIS.XY, op=ALU.add
-            )
-            inverse = small.tile([P, A, J_PASS], F32)
-            nc.vector.reciprocal(out=inverse[:], in_=total[:])
-            z_sb = work.tile([P, A, PACK, J_PASS, UH], BF16, tag="z_sb")
-            for a in range(A):
-                nc.gpsimd.tensor_tensor(
-                    out=z_sb[:, a, :, :, :],
-                    in0=e_sb[:, a, :, :, :],
-                    in1=inverse[:, a, :].unsqueeze(1).unsqueeze(3).to_broadcast([P, PACK, J_PASS, UH]),
-                    op=ALU.mult,
-                )
-            return z_sb
-
-        def quantise_z(z_sb, c):
-            grouped = work.tile([P, A, P, PACK], BF16, tag="grouped", align_bytes=64)
-            for pair in range(A // 2):
-                zt = psum_tr.tile([P, 2, PACK, P], BF16, tag="tr")
-                for ai in range(2):
-                    for t in range(PACK):
-                        nc.tensor.transpose(
-                            zt[:, ai, t, :],
-                            z_sb[:, 2 * pair + ai, t, :, :].rearrange("p j h -> p (j h)"),
-                            ident_bf[:],
-                        )
-                nc.scalar.copy(
-                    out=grouped[:, 2 * pair : 2 * pair + 2, :, :],
-                    in_=zt[:].rearrange("p a t b -> p a b t"),
-                )
-            nc.vector.quantize_mx(
-                out=z_codes[c][:].bitcast(FP8X4),
-                scales=z_scales[c][:],
-                in_=grouped[:].rearrange("p a b t -> p (a b t)"),
-            )
-
         def finish_rows(rt):
-            banks = [psum_scores.tile([P, A // 2, F], F32, name="scores%d" % half) for half in range(2)]
-            for a in range(A):
-                cols = slice(a * P, (a + 1) * P)
-                for c in range(N_PASS):
-                    nc.tensor.matmul_mx(
-                        out=banks[a // 4][:, a % 4, :],
-                        lhsT=z_codes[c][:, cols].bitcast(FP8X4),
-                        lhsT_scale=z_scales[c][:, cols],
-                        rhs=w_codes[c][:, cols].bitcast(FP8X4),
-                        rhs_scale=w_scales[c][:, cols],
-                        start=(c == 0),
-                        stop=(c == N_PASS - 1),
-                    )
-            top = small.tile([P, A], F32, tag="score_top")
-            for half in range(2):
-                nc.vector.tensor_reduce(
-                    out=top[:, half * 4 : half * 4 + 4], in_=banks[half][:], axis=AXIS.X, op=ALU.max
-                )
-            shift = small.tile([P, A], F32, tag="score_shift")
-            nc.vector.tensor_scalar(out=shift[:], in0=top[:], scalar1=-1.0 / J, scalar2=None, op0=ALU.mult)
             prob = work.tile([P, A, F], F32, tag="prob", bufs=1)
             total = small.tile([P, A], F32, tag="score_total")
-            for a in range(A):
-                nc.scalar.activation(
-                    out=prob[:, a, :],
-                    in_=banks[a // 4][:, a % 4, :],
-                    func=ACT.Exp,
-                    bias=shift[:, a : a + 1],
-                    scale=1.0 / J,
-                    accum_out=total[:, a : a + 1],
-                )
+            for half in range(2):
+                scores = psum_scores.tile([P, A // 2, F], F32)
+                for ai in range(A // 2):
+                    cols = slice((half * 4 + ai) * P, (half * 4 + ai + 1) * P)
+                    for c in range(N_PASS):
+                        nc.tensor.matmul_mx(
+                            out=scores[:, ai, :],
+                            lhsT=z_codes[c][:, cols].bitcast(FP8X4),
+                            lhsT_scale=z_scales[c][:, cols],
+                            rhs=w_codes[c][:, cols].bitcast(FP8X4),
+                            rhs_scale=w_scales[c][:, cols],
+                            start=(c == 0),
+                            stop=(c == N_PASS - 1),
+                        )
+                top = small.tile([P, A // 2], F32, tag="score_top")
+                nc.vector.tensor_reduce(out=top[:], in_=scores[:], axis=AXIS.X, op=ALU.max)
+                shift = small.tile([P, A // 2], F32, tag="score_shift")
+                nc.vector.tensor_scalar(out=shift[:], in0=top[:], scalar1=-1.0 / J, scalar2=None, op0=ALU.mult)
+                for ai in range(A // 2):
+                    a = half * 4 + ai
+                    nc.scalar.activation(
+                        out=prob[:, a, :],
+                        in_=scores[:, ai, :],
+                        func=ACT.Exp,
+                        bias=shift[:, ai : ai + 1],
+                        scale=1.0 / J,
+                        accum_out=total[:, a : a + 1],
+                    )
             inverse = small.tile([P, A], F32, tag="score_inverse")
             nc.vector.reciprocal(out=inverse[:], in_=total[:])
-            nc.vector.tensor_tensor(
+            nc.gpsimd.tensor_tensor(
                 out=prob[:], in0=prob[:], in1=inverse[:].unsqueeze(2).to_broadcast([P, A, F]), op=ALU.mult
             )
             nc.sync.dma_start(out=out[:, rt * P : (rt + 1) * P, :].rearrange("a b f -> b a f"), in_=prob[:])
 
-        waiting = None
-        for rt in range(ROW_TILES):
-            for c in range(N_PASS):
-                if rt == 0:
-                    load_kernels(c)
-                x_sb = load_xm(rt, c)
-                e_sb = exp_of_shifted_logits(x_sb, c)
-                if rt == 0:
-                    quantise_weights(c)
-                if waiting is not None:
-                    quantise_z(waiting[0], waiting[1])
-                    if waiting[1] == N_PASS - 1:
-                        finish_rows(waiting[2])
-                waiting = (normalise(e_sb), c, rt)
-        quantise_z(waiting[0], waiting[1])
-        finish_rows(waiting[2])
+        x_of = {}
+        xt_of = {}
+        e_of = {}
+        total_of = {}
+        z_of = {}
+        grouped_of = {}
+        x_of[0] = load(0)
+        x_of[1] = load(1)
+        xt_of[0] = transpose_xm(x_of[0])
+        for i in range(N_STEPS + 4):
+            if i + 2 < N_STEPS:
+                x_of[i + 2] = load(i + 2)
+            if i + 1 < N_STEPS:
+                xt_of[i + 1] = transpose_xm(x_of[i + 1])
+            if i < N_STEPS:
+                e_of[i] = work.tile([P, A, PACK, J_STEP, UH], F32, tag="e_sb", name="e_sb", bufs=4)
+                exp_of_shifted_logits(logits_and_max(i, xt_of[i], 0), e_of[i], 0)
+            if 0 <= i - 1 < N_STEPS:
+                pair_sum = add_word_halves(e_of[i - 1])
+            if 0 <= i - 2 < N_STEPS:
+                if (i - 2) % 2 == 0:
+                    z_of[(i - 2) // 2] = work.tile([P, A, PACK, J_PASS, UH], BF16, tag="z_sb", name="z_sb")
+                normalise(i - 2, e_of[i - 2], total_of[i - 2], z_of[(i - 2) // 2])
+            if i < N_STEPS:
+                exp_of_shifted_logits(logits_and_max(i, xt_of[i], 1), e_of[i], 1)
+            if 0 <= i - 1 < N_STEPS:
+                total_of[i - 1] = sum_of_units(pair_sum)
+            if 0 <= i - 4 < N_STEPS:
+                unit = (i - 4) // 2
+                rt, c, jl0 = place(i - 4)
+                if (i - 4) % 2 == 0:
+                    grouped_of[unit] = work.tile([P, A, P, PACK], BF16, tag="grouped", name="grouped", align_bytes=64)
+                    transpose_z(z_of[unit], grouped_of[unit], 0)
+                    transpose_z(z_of[unit], grouped_of[unit], 1)
+                else:
+                    transpose_z(z_of[unit], grouped_of[unit], 2)
+                    transpose_z(z_of[unit], grouped_of[unit], 3)
+                    nc.vector.quantize_mx(
+                        out=z_codes[c][:].bitcast(FP8X4),
+                        scales=z_scales[c][:],
+                        in_=grouped_of[unit][:].rearrange("p a b t -> p (a b t)"),
+                    )
+                    if rt == 0:
+                        quantise_weights(c)
+                    if c == N_PASS - 1:
+                        finish_rows(rt)

@@ -114,17 +114,10 @@ def tile_iterativefeatureexclusion_pa_kernel(tc, xm, kernels, out):
             quarter = e_sb[:, :, :, q * J_QUARTER : (q + 1) * J_QUARTER, :]
             nc.scalar.activation(out=quarter, in_=quarter, func=ACT.Exp)
 
-        def add_word_halves(e_sb):
-            pair_sum = work.tile([P, A, PACK // 2, J_STEP, UH], F32, tag="pair_sum")
-            nc.gpsimd.tensor_tensor(
-                out=pair_sum[:], in0=e_sb[:, :, 0 : PACK // 2, :, :], in1=e_sb[:, :, PACK // 2 : PACK, :, :], op=ALU.add
-            )
-            return pair_sum
-
-        def sum_of_units(pair_sum):
+        def sum_of_units(e_sb):
             total = small.tile([P, A, J_STEP], F32)
             nc.vector.tensor_reduce(
-                out=total[:], in_=pair_sum[:].rearrange("p a t j h -> p a j t h"), axis=AXIS.XY, op=ALU.add
+                out=total[:], in_=e_sb[:].rearrange("p a t j h -> p a j t h"), axis=AXIS.XY, op=ALU.add
             )
             return total
 
@@ -230,8 +223,6 @@ def tile_iterativefeatureexclusion_pa_kernel(tc, xm, kernels, out):
             if i < N_STEPS:
                 e_of[i] = work.tile([P, A, PACK, J_STEP, UH], F32, tag="e_sb", name="e_sb", bufs=4)
                 exp_of_shifted_logits(logits_and_max(i, xt_of[i], 0), e_of[i], 0)
-            if 0 <= i - 1 < N_STEPS:
-                pair_sum = add_word_halves(e_of[i - 1])
             if 0 <= i - 2 < N_STEPS:
                 if (i - 2) % 2 == 0:
                     z_of[(i - 2) // 2] = work.tile([P, A, PACK, J_PASS, UH], BF16, tag="z_sb", name="z_sb")
@@ -239,7 +230,7 @@ def tile_iterativefeatureexclusion_pa_kernel(tc, xm, kernels, out):
             if i < N_STEPS:
                 exp_of_shifted_logits(logits_and_max(i, xt_of[i], 1), e_of[i], 1)
             if 0 <= i - 1 < N_STEPS:
-                total_of[i - 1] = sum_of_units(pair_sum)
+                total_of[i - 1] = sum_of_units(e_of[i - 1])
             if 0 <= i - 4 < N_STEPS:
                 unit = (i - 4) // 2
                 rt, c, jl0 = place(i - 4)

@@ -26,6 +26,7 @@ ROW_TILES = B // P
 J_STEP = J_PASS // 2
 J_QUARTER = 4
 J_BANK = 2
+J_VECTOR = 6
 N_STEPS = ROW_TILES * J // J_STEP
 
 FLOPS = 2 * J * B * F * A * U + 2 * A * B * J * U * F
@@ -96,35 +97,50 @@ def tile_iterativefeatureexclusion_pa_kernel(tc, xm, kernels, out):
                         start=True,
                         stop=True,
                     )
-                top = small.tile([P, J_BANK, A], F32)
-                nc.vector.tensor_reduce(out=top[:], in_=logits[:], axis=AXIS.X, op=ALU.max)
-                banks.append((logits, top))
+                shift = small.tile([P, J_BANK, A], F32)
+                nc.vector.tensor_reduce(out=shift[:], in_=logits[:], axis=AXIS.X, op=ALU.max, negate=True)
+                banks.append((logits, shift, js0))
             return banks
 
-        def exp_of_shifted_logits(banks, e_sb, q):
-            for half in range(J_QUARTER // J_BANK):
-                logits, top = banks[half]
-                js0 = q * J_QUARTER + half * J_BANK
+        def exp_by_vector_and_scalar(banks, e_sb):
+            for logits, shift, js0 in banks:
                 nc.vector.tensor_tensor(
                     out=e_sb[:, :, :, js0 : js0 + J_BANK, :].rearrange("p a t j h -> p j a t h"),
                     in0=logits[:].rearrange("p j a (h t) -> p j a t h", t=PACK),
-                    in1=top[:].unsqueeze(3).unsqueeze(4).to_broadcast([P, J_BANK, A, PACK, UH]),
-                    op=ALU.subtract,
+                    in1=shift[:].unsqueeze(3).unsqueeze(4).to_broadcast([P, J_BANK, A, PACK, UH]),
+                    op=ALU.add,
                 )
-            quarter = e_sb[:, :, :, q * J_QUARTER : (q + 1) * J_QUARTER, :]
-            nc.scalar.activation(out=quarter, in_=quarter, func=ACT.Exp)
+            first = banks[0][2]
+            done = e_sb[:, :, :, first : first + J_BANK * len(banks), :]
+            nc.scalar.activation(out=done, in_=done, func=ACT.Exp)
+
+        def exp_by_scalar_alone(bank, e_sb, total_sc):
+            logits, shift, js0 = bank
+            for i in range(J_BANK):
+                for a in range(A):
+                    nc.scalar.activation(
+                        out=e_sb[:, a, :, js0 + i, :],
+                        in_=logits[:, i, a, :].rearrange("p (h t) -> p t h", t=PACK),
+                        func=ACT.Exp,
+                        bias=shift[:, i, a : a + 1],
+                        accum_out=total_sc[:, a, i : i + 1],
+                    )
 
         def sum_of_units(e_sb):
-            total = small.tile([P, A, J_STEP], F32)
+            total = small.tile([P, A, J_VECTOR], F32)
             nc.vector.tensor_reduce(
-                out=total[:], in_=e_sb[:].rearrange("p a t j h -> p a j t h"), axis=AXIS.XY, op=ALU.add
+                out=total[:],
+                in_=e_sb[:, :, :, 0:J_VECTOR, :].rearrange("p a t j h -> p a j t h"),
+                axis=AXIS.XY,
+                op=ALU.add,
             )
             return total
 
-        def normalise(step, e_sb, total, z_sb):
+        def normalise(step, e_sb, total, total_sc, z_sb):
             rt, c, jl0 = place(step)
             inverse = small.tile([P, A, J_STEP], F32)
-            nc.vector.reciprocal(out=inverse[:], in_=total[:])
+            nc.vector.reciprocal(out=inverse[:, :, 0:J_VECTOR], in_=total[:])
+            nc.vector.reciprocal(out=inverse[:, :, J_VECTOR:J_STEP], in_=total_sc[:])
             nc.gpsimd.tensor_tensor(
                 out=z_sb[:, :, :, jl0 : jl0 + J_STEP, :].rearrange("p a t j h -> p t a j h"),
                 in0=e_sb[:].rearrange("p a t j h -> p t a j h"),
@@ -210,6 +226,7 @@ def tile_iterativefeatureexclusion_pa_kernel(tc, xm, kernels, out):
         xt_of = {}
         e_of = {}
         total_of = {}
+        total_sc_of = {}
         z_of = {}
         grouped_of = {}
         x_of[0] = load(0)
@@ -222,13 +239,16 @@ def tile_iterativefeatureexclusion_pa_kernel(tc, xm, kernels, out):
                 xt_of[i + 1] = transpose_xm(x_of[i + 1])
             if i < N_STEPS:
                 e_of[i] = work.tile([P, A, PACK, J_STEP, UH], F32, tag="e_sb", name="e_sb", bufs=4)
-                exp_of_shifted_logits(logits_and_max(i, xt_of[i], 0), e_of[i], 0)
+                exp_by_vector_and_scalar(logits_and_max(i, xt_of[i], 0), e_of[i])
             if 0 <= i - 2 < N_STEPS:
                 if (i - 2) % 2 == 0:
                     z_of[(i - 2) // 2] = work.tile([P, A, PACK, J_PASS, UH], BF16, tag="z_sb", name="z_sb")
-                normalise(i - 2, e_of[i - 2], total_of[i - 2], z_of[(i - 2) // 2])
+                normalise(i - 2, e_of[i - 2], total_of[i - 2], total_sc_of[i - 2], z_of[(i - 2) // 2])
             if i < N_STEPS:
-                exp_of_shifted_logits(logits_and_max(i, xt_of[i], 1), e_of[i], 1)
+                banks = logits_and_max(i, xt_of[i], 1)
+                exp_by_vector_and_scalar(banks[0:1], e_of[i])
+                total_sc_of[i] = small.tile([P, A, J_STEP - J_VECTOR], F32, tag="total_sc", name="total_sc")
+                exp_by_scalar_alone(banks[1], e_of[i], total_sc_of[i])
             if 0 <= i - 1 < N_STEPS:
                 total_of[i - 1] = sum_of_units(e_of[i - 1])
             if 0 <= i - 4 < N_STEPS:

@@ -26,7 +26,6 @@ ROW_TILES = B // P
 J_STEP = J_PASS // 2
 J_QUARTER = 4
 J_BANK = 2
-J_VECTOR = 6
 N_STEPS = ROW_TILES * J // J_STEP
 
 FLOPS = 2 * J * B * F * A * U + 2 * A * B * J * U * F
@@ -41,8 +40,7 @@ def tile_iterativefeatureexclusion_pa_kernel(tc, xm, kernels, out):
         work = ctx.enter_context(tc.tile_pool(name="work", bufs=2))
         small = ctx.enter_context(tc.tile_pool(name="small", bufs=4))
         psum_logits = ctx.enter_context(tc.psum_pool(name="psum_logits", bufs=4))
-        psum_tr = ctx.enter_context(tc.psum_pool(name="psum_tr", bufs=3))
-        psum_scores = ctx.enter_context(tc.psum_pool(name="psum_scores", bufs=1))
+        psum_tr = ctx.enter_context(tc.psum_pool(name="psum_tr", bufs=4))
 
         ident_bf = const.tile([P, P], BF16)
         make_identity(nc, ident_bf[:])
@@ -87,63 +85,70 @@ def tile_iterativefeatureexclusion_pa_kernel(tc, xm, kernels, out):
             rt, c, jl0 = place(step)
             banks = []
             for half in range(J_QUARTER // J_BANK):
-                logits = psum_logits.tile([P, J_BANK, A, U], F32)
+                logits = psum_logits.tile([P, A, J_BANK, U], F32)
                 js0 = q * J_QUARTER + half * J_BANK
                 for i in range(J_BANK):
                     nc.tensor.matmul(
-                        out=logits[:, i, :, :],
+                        out=logits[:, :, i, :],
                         lhsT=xt_sb[:, js0 + i, :],
                         rhs=k_sb[c][:, :, jl0 + js0 + i, :],
                         start=True,
                         stop=True,
                     )
-                shift = small.tile([P, J_BANK, A], F32)
-                nc.vector.tensor_reduce(out=shift[:], in_=logits[:], axis=AXIS.X, op=ALU.max, negate=True)
-                banks.append((logits, shift, js0))
+                top = small.tile([P, A, J_BANK], F32)
+                nc.vector.tensor_reduce(out=top[:], in_=logits[:], axis=AXIS.X, op=ALU.max)
+                banks.append((logits, top))
             return banks
 
-        def exp_by_vector_and_scalar(banks, e_sb):
-            for logits, shift, js0 in banks:
+        def exp_of_shifted_logits(banks, e_sb, q):
+            for half in range(J_QUARTER // J_BANK):
+                logits, top = banks[half]
+                js0 = q * J_QUARTER + half * J_BANK
                 nc.vector.tensor_tensor(
-                    out=e_sb[:, :, :, js0 : js0 + J_BANK, :].rearrange("p a t j h -> p j a t h"),
-                    in0=logits[:].rearrange("p j a (h t) -> p j a t h", t=PACK),
-                    in1=shift[:].unsqueeze(3).unsqueeze(4).to_broadcast([P, J_BANK, A, PACK, UH]),
-                    op=ALU.add,
+                    out=e_sb[:, :, :, js0 : js0 + J_BANK, :],
+                    in0=logits[:].rearrange("p a j (h t) -> p t a j h", t=PACK),
+                    in1=top[:].unsqueeze(1).unsqueeze(4).to_broadcast([P, PACK, A, J_BANK, UH]),
+                    op=ALU.subtract,
                 )
-            first = banks[0][2]
-            done = e_sb[:, :, :, first : first + J_BANK * len(banks), :]
-            nc.scalar.activation(out=done, in_=done, func=ACT.Exp)
+            quarter = e_sb[:, :, :, q * J_QUARTER : (q + 1) * J_QUARTER, :]
+            nc.scalar.activation(out=quarter, in_=quarter, func=ACT.Exp)
 
-        def exp_by_scalar_alone(bank, e_sb, total_sc):
-            logits, shift, js0 = bank
-            for i in range(J_BANK):
-                for a in range(A):
-                    nc.scalar.activation(
-                        out=e_sb[:, a, :, js0 + i, :],
-                        in_=logits[:, i, a, :].rearrange("p (h t) -> p t h", t=PACK),
-                        func=ACT.Exp,
-                        bias=shift[:, i, a : a + 1],
-                        accum_out=total_sc[:, a, i : i + 1],
+        def add_word_places(e_sb):
+            added = psum_tr.tile([P, A // 2, P], F32, tag="tr")
+            for pair in range(A // 2):
+                for t in range(PACK):
+                    nc.tensor.matmul(
+                        out=added[:, pair, :],
+                        lhsT=e_sb[:, t, 2 * pair : 2 * pair + 2, :, :].rearrange("p a j h -> p (a j h)"),
+                        rhs=ident_f32[:],
+                        is_transpose=True,
+                        start=(t == 0),
+                        stop=(t == PACK - 1),
                     )
+            part = work.tile([P, A // 2, P], F32, tag="part")
+            nc.scalar.copy(out=part[:], in_=added[:])
+            return part
 
-        def sum_of_units(e_sb):
-            total = small.tile([P, A, J_VECTOR], F32)
+        def sum_of_units(part):
+            back = psum_tr.tile([P, A // 2, P], F32, tag="tr")
+            for pair in range(A // 2):
+                nc.tensor.transpose(back[:, pair, :], part[:, pair, :], ident_f32[:])
+            total = small.tile([P, A, J_STEP], F32)
             nc.vector.tensor_reduce(
-                out=total[:],
-                in_=e_sb[:, :, :, 0:J_VECTOR, :].rearrange("p a t j h -> p a j t h"),
-                axis=AXIS.XY,
+                out=total[:].rearrange("p a j -> p (a j)"),
+                in_=back[:].rearrange("p q (g h) -> p (q g) h", h=UH),
+                axis=AXIS.X,
                 op=ALU.add,
             )
             return total
 
-        def normalise(step, e_sb, total, total_sc, z_sb):
+        def normalise(step, e_sb, total, z_sb):
             rt, c, jl0 = place(step)
             inverse = small.tile([P, A, J_STEP], F32)
-            nc.vector.reciprocal(out=inverse[:, :, 0:J_VECTOR], in_=total[:])
-            nc.vector.reciprocal(out=inverse[:, :, J_VECTOR:J_STEP], in_=total_sc[:])
+            nc.vector.reciprocal(out=inverse[:], in_=total[:])
             nc.gpsimd.tensor_tensor(
                 out=z_sb[:, :, :, jl0 : jl0 + J_STEP, :].rearrange("p a t j h -> p t a j h"),
-                in0=e_sb[:].rearrange("p a t j h -> p t a j h"),
+                in0=e_sb[:],
                 in1=inverse[:].unsqueeze(1).unsqueeze(4).to_broadcast([P, PACK, A, J_STEP, UH]),
                 op=ALU.mult,
             )
@@ -188,7 +193,7 @@ def tile_iterativefeatureexclusion_pa_kernel(tc, xm, kernels, out):
             prob = work.tile([P, A, F], F32, tag="prob", bufs=1)
             total = small.tile([P, A], F32, tag="score_total")
             for half in range(2):
-                scores = psum_scores.tile([P, A // 2, F], F32)
+                scores = psum_tr.tile([P, A // 2, F], F32, tag="tr")
                 for ai in range(A // 2):
                     cols = slice((half * 4 + ai) * P, (half * 4 + ai + 1) * P)
                     for c in range(N_PASS):
@@ -226,7 +231,6 @@ def tile_iterativefeatureexclusion_pa_kernel(tc, xm, kernels, out):
         xt_of = {}
         e_of = {}
         total_of = {}
-        total_sc_of = {}
         z_of = {}
         grouped_of = {}
         x_of[0] = load(0)
@@ -238,19 +242,18 @@ def tile_iterativefeatureexclusion_pa_kernel(tc, xm, kernels, out):
             if i + 1 < N_STEPS:
                 xt_of[i + 1] = transpose_xm(x_of[i + 1])
             if i < N_STEPS:
-                e_of[i] = work.tile([P, A, PACK, J_STEP, UH], F32, tag="e_sb", name="e_sb", bufs=4)
-                exp_by_vector_and_scalar(logits_and_max(i, xt_of[i], 0), e_of[i])
+                e_of[i] = work.tile([P, PACK, A, J_STEP, UH], F32, tag="e_sb", name="e_sb", bufs=4)
+                exp_of_shifted_logits(logits_and_max(i, xt_of[i], 0), e_of[i], 0)
+            if 0 <= i - 1 < N_STEPS:
+                part = add_word_places(e_of[i - 1])
             if 0 <= i - 2 < N_STEPS:
                 if (i - 2) % 2 == 0:
                     z_of[(i - 2) // 2] = work.tile([P, A, PACK, J_PASS, UH], BF16, tag="z_sb", name="z_sb")
-                normalise(i - 2, e_of[i - 2], total_of[i - 2], total_sc_of[i - 2], z_of[(i - 2) // 2])
+                normalise(i - 2, e_of[i - 2], total_of[i - 2], z_of[(i - 2) // 2])
             if i < N_STEPS:
-                banks = logits_and_max(i, xt_of[i], 1)
-                exp_by_vector_and_scalar(banks[0:1], e_of[i])
-                total_sc_of[i] = small.tile([P, A, J_STEP - J_VECTOR], F32, tag="total_sc", name="total_sc")
-                exp_by_scalar_alone(banks[1], e_of[i], total_sc_of[i])
+                exp_of_shifted_logits(logits_and_max(i, xt_of[i], 1), e_of[i], 1)
             if 0 <= i - 1 < N_STEPS:
-                total_of[i - 1] = sum_of_units(e_of[i - 1])
+                total_of[i - 1] = sum_of_units(part)
             if 0 <= i - 4 < N_STEPS:
                 unit = (i - 4) // 2
                 rt, c, jl0 = place(i - 4)

@@ -26,6 +26,7 @@ ROW_TILES = B // P
 J_STEP = J_PASS // 2
 J_QUARTER = 4
 J_BANK = 2
+J_VECTOR = 6
 N_STEPS = ROW_TILES * J // J_STEP
 
 FLOPS = 2 * J * B * F * A * U + 2 * A * B * J * U * F
@@ -78,77 +79,73 @@ def tile_iterativefeatureexclusion_pa_kernel(tc, xm, kernels, out):
                 xt_ps = psum_tr.tile([P, J_QUARTER, P], BF16, tag="tr")
                 for i in range(J_QUARTER):
                     nc.tensor.transpose(xt_ps[:, i, :], x_sb[:, q * J_QUARTER + i, :], ident_bf[:])
-                nc.scalar.copy(out=xt_sb[:, js, :], in_=xt_ps[:])
+                if q == 0:
+                    nc.scalar.copy(out=xt_sb[:, js, :], in_=xt_ps[:])
+                else:
+                    nc.vector.tensor_copy(out=xt_sb[:, js, :], in_=xt_ps[:])
             return xt_sb
 
         def logits_and_max(step, xt_sb, q):
             rt, c, jl0 = place(step)
             banks = []
             for half in range(J_QUARTER // J_BANK):
-                logits = psum_logits.tile([P, A, J_BANK, U], F32)
+                logits = psum_logits.tile([P, J_BANK, A, U], F32)
                 js0 = q * J_QUARTER + half * J_BANK
                 for i in range(J_BANK):
                     nc.tensor.matmul(
-                        out=logits[:, :, i, :],
+                        out=logits[:, i, :, :],
                         lhsT=xt_sb[:, js0 + i, :],
                         rhs=k_sb[c][:, :, jl0 + js0 + i, :],
                         start=True,
                         stop=True,
                     )
-                top = small.tile([P, A, J_BANK], F32)
-                nc.vector.tensor_reduce(out=top[:], in_=logits[:], axis=AXIS.X, op=ALU.max)
-                banks.append((logits, top))
+                shift = small.tile([P, J_BANK, A], F32)
+                nc.vector.tensor_reduce(out=shift[:], in_=logits[:], axis=AXIS.X, op=ALU.max, negate=True)
+                banks.append((logits, shift, js0))
             return banks
 
-        def exp_of_shifted_logits(banks, e_sb, q):
-            for half in range(J_QUARTER // J_BANK):
-                logits, top = banks[half]
-                js0 = q * J_QUARTER + half * J_BANK
+        def exp_by_vector_and_scalar(banks, e_sb):
+            for logits, shift, js0 in banks:
                 nc.vector.tensor_tensor(
-                    out=e_sb[:, :, :, js0 : js0 + J_BANK, :],
-                    in0=logits[:].rearrange("p a j (h t) -> p t a j h", t=PACK),
-                    in1=top[:].unsqueeze(1).unsqueeze(4).to_broadcast([P, PACK, A, J_BANK, UH]),
-                    op=ALU.subtract,
+                    out=e_sb[:, :, :, js0 : js0 + J_BANK, :].rearrange("p a t j h -> p j a t h"),
+                    in0=logits[:].rearrange("p j a (h t) -> p j a t h", t=PACK),
+                    in1=shift[:].unsqueeze(3).unsqueeze(4).to_broadcast([P, J_BANK, A, PACK, UH]),
+                    op=ALU.add,
                 )
-            quarter = e_sb[:, :, :, q * J_QUARTER : (q + 1) * J_QUARTER, :]
-            nc.scalar.activation(out=quarter, in_=quarter, func=ACT.Exp)
+            first = banks[0][2]
+            done = e_sb[:, :, :, first : first + J_BANK * len(banks), :]
+            nc.scalar.activation(out=done, in_=done, func=ACT.Exp)
 
-        def add_word_places(e_sb):
-            added = psum_tr.tile([P, A // 2, P], F32, tag="tr")
-            for pair in range(A // 2):
-                for t in range(PACK):
-                    nc.tensor.matmul(
-                        out=added[:, pair, :],
-                        lhsT=e_sb[:, t, 2 * pair : 2 * pair + 2, :, :].rearrange("p a j h -> p (a j h)"),
-                        rhs=ident_f32[:],
-                        is_transpose=True,
-                        start=(t == 0),
-                        stop=(t == PACK - 1),
+        def exp_by_scalar_alone(bank, e_sb, total_sc):
+            logits, shift, js0 = bank
+            for i in range(J_BANK):
+                for a in range(A):
+                    nc.scalar.activation(
+                        out=e_sb[:, a, :, js0 + i, :],
+                        in_=logits[:, i, a, :].rearrange("p (h t) -> p t h", t=PACK),
+                        func=ACT.Exp,
+                        bias=shift[:, i, a : a + 1],
+                        accum_out=total_sc[:, a, i : i + 1],
                     )
-            part = work.tile([P, A // 2, P], F32, tag="part")
-            nc.scalar.copy(out=part[:], in_=added[:])
-            return part
 
-        def sum_of_units(part):
-            back = psum_tr.tile([P, A // 2, P], F32, tag="tr")
-            for pair in range(A // 2):
-                nc.tensor.transpose(back[:, pair, :], part[:, pair, :], ident_f32[:])
-            total = small.tile([P, A, J_STEP], F32)
+        def sum_of_units(e_sb):
+            total = small.tile([P, A, J_VECTOR], F32)
             nc.vector.tensor_reduce(
-                out=total[:].rearrange("p a j -> p (a j)"),
-                in_=back[:].rearrange("p q (g h) -> p (q g) h", h=UH),
-                axis=AXIS.X,
+                out=total[:],
+                in_=e_sb[:, :, :, 0:J_VECTOR, :].rearrange("p a t j h -> p a j t h"),
+                axis=AXIS.XY,
                 op=ALU.add,
             )
             return total
 
-        def normalise(step, e_sb, total, z_sb):
+        def normalise(step, e_sb, total, total_sc, z_sb):
             rt, c, jl0 = place(step)
             inverse = small.tile([P, A, J_STEP], F32)
-            nc.vector.reciprocal(out=inverse[:], in_=total[:])
+            nc.vector.reciprocal(out=inverse[:, :, 0:J_VECTOR], in_=total[:])
+            nc.vector.reciprocal(out=inverse[:, :, J_VECTOR:J_STEP], in_=total_sc[:])
             nc.gpsimd.tensor_tensor(
                 out=z_sb[:, :, :, jl0 : jl0 + J_STEP, :].rearrange("p a t j h -> p t a j h"),
-                in0=e_sb[:],
+                in0=e_sb[:].rearrange("p a t j h -> p t a j h"),
                 in1=inverse[:].unsqueeze(1).unsqueeze(4).to_broadcast([P, PACK, A, J_STEP, UH]),
                 op=ALU.mult,
             )
@@ -231,6 +228,7 @@ def tile_iterativefeatureexclusion_pa_kernel(tc, xm, kernels, out):
         xt_of = {}
         e_of = {}
         total_of = {}
+        total_sc_of = {}
         z_of = {}
         grouped_of = {}
         x_of[0] = load(0)
@@ -242,18 +240,19 @@ def tile_iterativefeatureexclusion_pa_kernel(tc, xm, kernels, out):
             if i + 1 < N_STEPS:
                 xt_of[i + 1] = transpose_xm(x_of[i + 1])
             if i < N_STEPS:
-                e_of[i] = work.tile([P, PACK, A, J_STEP, UH], F32, tag="e_sb", name="e_sb", bufs=4)
-                exp_of_shifted_logits(logits_and_max(i, xt_of[i], 0), e_of[i], 0)
-            if 0 <= i - 1 < N_STEPS:
-                part = add_word_places(e_of[i - 1])
+                e_of[i] = work.tile([P, A, PACK, J_STEP, UH], F32, tag="e_sb", name="e_sb", bufs=4)
+                exp_by_vector_and_scalar(logits_and_max(i, xt_of[i], 0), e_of[i])
             if 0 <= i - 2 < N_STEPS:
                 if (i - 2) % 2 == 0:
                     z_of[(i - 2) // 2] = work.tile([P, A, PACK, J_PASS, UH], BF16, tag="z_sb", name="z_sb")
-                normalise(i - 2, e_of[i - 2], total_of[i - 2], z_of[(i - 2) // 2])
+                normalise(i - 2, e_of[i - 2], total_of[i - 2], total_sc_of[i - 2], z_of[(i - 2) // 2])
             if i < N_STEPS:
-                exp_of_shifted_logits(logits_and_max(i, xt_of[i], 1), e_of[i], 1)
+                banks = logits_and_max(i, xt_of[i], 1)
+                exp_by_vector_and_scalar(banks[0:1], e_of[i])
+                total_sc_of[i] = small.tile([P, A, J_STEP - J_VECTOR], F32, tag="total_sc", name="total_sc")
+                exp_by_scalar_alone(banks[1], e_of[i], total_sc_of[i])
             if 0 <= i - 1 < N_STEPS:
-                total_of[i - 1] = sum_of_units(part)
+                total_of[i - 1] = sum_of_units(e_of[i - 1])
             if 0 <= i - 4 < N_STEPS:
                 unit = (i - 4) // 2
                 rt, c, jl0 = place(i - 4)

@@ -20,6 +20,7 @@ A = 8
 U = 32
 PACK = 4
 UH = U // PACK
+H = 2
 J_PASS = P // UH
 N_PASS = J // J_PASS
 ROW_TILES = B // P
@@ -79,10 +80,7 @@ def tile_iterativefeatureexclusion_pa_kernel(tc, xm, kernels, out):
                 xt_ps = psum_tr.tile([P, J_QUARTER, P], BF16, tag="tr")
                 for i in range(J_QUARTER):
                     nc.tensor.transpose(xt_ps[:, i, :], x_sb[:, q * J_QUARTER + i, :], ident_bf[:])
-                if q == 0:
-                    nc.scalar.copy(out=xt_sb[:, js, :], in_=xt_ps[:])
-                else:
-                    nc.vector.tensor_copy(out=xt_sb[:, js, :], in_=xt_ps[:])
+                nc.scalar.copy(out=xt_sb[:, js, :], in_=xt_ps[:])
             return xt_sb
 
         def logits_and_max(step, xt_sb, q):
@@ -107,60 +105,54 @@ def tile_iterativefeatureexclusion_pa_kernel(tc, xm, kernels, out):
         def exp_by_vector_and_scalar(banks, e_sb):
             for logits, shift, js0 in banks:
                 nc.vector.tensor_tensor(
-                    out=e_sb[:, :, :, js0 : js0 + J_BANK, :].rearrange("p a t j h -> p j a t h"),
-                    in0=logits[:].rearrange("p j a (h t) -> p j a t h", t=PACK),
-                    in1=shift[:].unsqueeze(3).unsqueeze(4).to_broadcast([P, J_BANK, A, PACK, UH]),
+                    out=e_sb[:, :, js0 : js0 + J_BANK, :].rearrange("p a j u -> p j a u"),
+                    in0=logits[:],
+                    in1=shift[:].unsqueeze(3).to_broadcast([P, J_BANK, A, U]),
                     op=ALU.add,
                 )
             first = banks[0][2]
-            done = e_sb[:, :, :, first : first + J_BANK * len(banks), :]
+            done = e_sb[:, :, first : first + J_BANK * len(banks), :]
             nc.scalar.activation(out=done, in_=done, func=ACT.Exp)
 
-        def exp_by_scalar_alone(bank, e_sb, total_sc):
+        def exp_by_scalar_alone(bank, e_sb, total):
             logits, shift, js0 = bank
             for i in range(J_BANK):
                 for a in range(A):
                     nc.scalar.activation(
-                        out=e_sb[:, a, :, js0 + i, :],
-                        in_=logits[:, i, a, :].rearrange("p (h t) -> p t h", t=PACK),
+                        out=e_sb[:, a, js0 + i, :],
+                        in_=logits[:, i, a, :],
                         func=ACT.Exp,
                         bias=shift[:, i, a : a + 1],
-                        accum_out=total_sc[:, a, i : i + 1],
+                        accum_out=total[:, a, js0 + i : js0 + i + 1],
                     )
 
-        def sum_of_units(e_sb):
-            total = small.tile([P, A, J_VECTOR], F32)
+        def sum_of_units(e_sb, total):
             nc.vector.tensor_reduce(
-                out=total[:],
-                in_=e_sb[:, :, :, 0:J_VECTOR, :].rearrange("p a t j h -> p a j t h"),
-                axis=AXIS.XY,
-                op=ALU.add,
+                out=total[:, :, 0:J_VECTOR], in_=e_sb[:, :, 0:J_VECTOR, :], axis=AXIS.X, op=ALU.add
             )
-            return total
 
-        def normalise(step, e_sb, total, total_sc, z_sb):
+        def normalise(step, e_sb, total, z_sb):
             rt, c, jl0 = place(step)
             inverse = small.tile([P, A, J_STEP], F32)
-            nc.vector.reciprocal(out=inverse[:, :, 0:J_VECTOR], in_=total[:])
-            nc.vector.reciprocal(out=inverse[:, :, J_VECTOR:J_STEP], in_=total_sc[:])
+            nc.vector.reciprocal(out=inverse[:], in_=total[:])
             nc.gpsimd.tensor_tensor(
-                out=z_sb[:, :, :, jl0 : jl0 + J_STEP, :].rearrange("p a t j h -> p t a j h"),
-                in0=e_sb[:].rearrange("p a t j h -> p t a j h"),
-                in1=inverse[:].unsqueeze(1).unsqueeze(4).to_broadcast([P, PACK, A, J_STEP, UH]),
+                out=z_sb[:, :, jl0 : jl0 + J_STEP, :],
+                in0=e_sb[:],
+                in1=inverse[:].unsqueeze(3).to_broadcast([P, A, J_STEP, U]),
                 op=ALU.mult,
             )
 
         def transpose_z(z_sb, grouped, pair):
-            zt = psum_tr.tile([P, 2, PACK, P], BF16, tag="tr")
+            zt = psum_tr.tile([P, 2, H, P], F32, tag="tr")
             for ai in range(2):
-                for t in range(PACK):
+                words = z_sb[:, 2 * pair + ai, :, :].rearrange("p j u -> p (j u)").bitcast(F32)
+                for h in range(H):
                     nc.tensor.transpose(
-                        zt[:, ai, t, :],
-                        z_sb[:, 2 * pair + ai, t, :, :].rearrange("p j h -> p (j h)"),
-                        ident_bf[:],
+                        zt[:, ai, h, :], words.rearrange("p (w h) -> p w h", h=H)[:, :, h], ident_f32[:]
                     )
             nc.scalar.copy(
-                out=grouped[:, 2 * pair : 2 * pair + 2, :, :], in_=zt[:].rearrange("p a t b -> p a b t")
+                out=grouped[:, 2 * pair : 2 * pair + 2, :, :].rearrange("p a b t -> p (a b t)").bitcast(F32),
+                in_=zt[:].rearrange("p a h b -> p a b h"),
             )
 
         def quantise_weights(c):
@@ -228,7 +220,6 @@ def tile_iterativefeatureexclusion_pa_kernel(tc, xm, kernels, out):
         xt_of = {}
         e_of = {}
         total_of = {}
-        total_sc_of = {}
         z_of = {}
         grouped_of = {}
         x_of[0] = load(0)
@@ -240,19 +231,19 @@ def tile_iterativefeatureexclusion_pa_kernel(tc, xm, kernels, out):
             if i + 1 < N_STEPS:
                 xt_of[i + 1] = transpose_xm(x_of[i + 1])
             if i < N_STEPS:
-                e_of[i] = work.tile([P, A, PACK, J_STEP, UH], F32, tag="e_sb", name="e_sb", bufs=4)
+                e_of[i] = work.tile([P, A, J_STEP, U], F32, tag="e_sb", name="e_sb", bufs=4)
                 exp_by_vector_and_scalar(logits_and_max(i, xt_of[i], 0), e_of[i])
             if 0 <= i - 2 < N_STEPS:
                 if (i - 2) % 2 == 0:
-                    z_of[(i - 2) // 2] = work.tile([P, A, PACK, J_PASS, UH], BF16, tag="z_sb", name="z_sb")
-                normalise(i - 2, e_of[i - 2], total_of[i - 2], total_sc_of[i - 2], z_of[(i - 2) // 2])
+                    z_of[(i - 2) // 2] = work.tile([P, A, J_PASS, U], BF16, tag="z_sb", name="z_sb")
+                normalise(i - 2, e_of[i - 2], total_of[i - 2], z_of[(i - 2) // 2])
             if i < N_STEPS:
                 banks = logits_and_max(i, xt_of[i], 1)
                 exp_by_vector_and_scalar(banks[0:1], e_of[i])
-                total_sc_of[i] = small.tile([P, A, J_STEP - J_VECTOR], F32, tag="total_sc", name="total_sc")
-                exp_by_scalar_alone(banks[1], e_of[i], total_sc_of[i])
+                total_of[i] = small.tile([P, A, J_STEP], F32, tag="total", name="total")
+                exp_by_scalar_alone(banks[1], e_of[i], total_of[i])
             if 0 <= i - 1 < N_STEPS:
-                total_of[i - 1] = sum_of_units(e_of[i - 1])
+                sum_of_units(e_of[i - 1], total_of[i - 1])
             if 0 <= i - 4 < N_STEPS:
                 unit = (i - 4) // 2
                 rt, c, jl0 = place(i - 4)

@@ -27,7 +27,7 @@ ROW_TILES = B // P
 J_STEP = J_PASS // 2
 J_QUARTER = 4
 J_BANK = 2
-J_VECTOR = 6
+J_VECTOR = 5
 N_STEPS = ROW_TILES * J // J_STEP
 
 FLOPS = 2 * J * B * F * A * U + 2 * A * B * J * U * F
@@ -102,29 +102,32 @@ def tile_iterativefeatureexclusion_pa_kernel(tc, xm, kernels, out):
                 banks.append((logits, shift, js0))
             return banks
 
-        def exp_by_vector_and_scalar(banks, e_sb):
-            for logits, shift, js0 in banks:
-                nc.vector.tensor_tensor(
-                    out=e_sb[:, :, js0 : js0 + J_BANK, :].rearrange("p a j u -> p j a u"),
-                    in0=logits[:],
-                    in1=shift[:].unsqueeze(3).to_broadcast([P, J_BANK, A, U]),
-                    op=ALU.add,
-                )
+        def exponentials(banks, e_sb, total):
             first = banks[0][2]
-            done = e_sb[:, :, first : first + J_BANK * len(banks), :]
-            nc.scalar.activation(out=done, in_=done, func=ACT.Exp)
-
-        def exp_by_scalar_alone(bank, e_sb, total):
-            logits, shift, js0 = bank
-            for i in range(J_BANK):
-                for a in range(A):
-                    nc.scalar.activation(
-                        out=e_sb[:, a, js0 + i, :],
-                        in_=logits[:, i, a, :],
-                        func=ACT.Exp,
-                        bias=shift[:, i, a : a + 1],
-                        accum_out=total[:, a, js0 + i : js0 + i + 1],
+            last = min(first + J_QUARTER, J_VECTOR)
+            for logits, shift, js0 in banks:
+                n = min(J_BANK, J_VECTOR - js0)
+                if n > 0:
+                    nc.vector.tensor_tensor(
+                        out=e_sb[:, :, js0 : js0 + n, :].rearrange("p a j u -> p j a u"),
+                        in0=logits[:, 0:n, :, :],
+                        in1=shift[:, 0:n, :].unsqueeze(3).to_broadcast([P, n, A, U]),
+                        op=ALU.add,
                     )
+            if last > first:
+                done = e_sb[:, :, first:last, :]
+                nc.scalar.activation(out=done, in_=done, func=ACT.Exp)
+            for logits, shift, js0 in banks:
+                for i in range(J_BANK):
+                    if js0 + i >= J_VECTOR:
+                        for a in range(A):
+                            nc.scalar.activation(
+                                out=e_sb[:, a, js0 + i, :],
+                                in_=logits[:, i, a, :],
+                                func=ACT.Exp,
+                                bias=shift[:, i, a : a + 1],
+                                accum_out=total[:, a, js0 + i : js0 + i + 1],
+                            )
 
         def sum_of_units(e_sb, total):
             nc.vector.tensor_reduce(
@@ -232,16 +235,14 @@ def tile_iterativefeatureexclusion_pa_kernel(tc, xm, kernels, out):
                 xt_of[i + 1] = transpose_xm(x_of[i + 1])
             if i < N_STEPS:
                 e_of[i] = work.tile([P, A, J_STEP, U], F32, tag="e_sb", name="e_sb", bufs=4)
-                exp_by_vector_and_scalar(logits_and_max(i, xt_of[i], 0), e_of[i])
+                total_of[i] = small.tile([P, A, J_STEP], F32, tag="total", name="total")
+                exponentials(logits_and_max(i, xt_of[i], 0), e_of[i], total_of[i])
             if 0 <= i - 2 < N_STEPS:
                 if (i - 2) % 2 == 0:
                     z_of[(i - 2) // 2] = work.tile([P, A, J_PASS, U], BF16, tag="z_sb", name="z_sb")
                 normalise(i - 2, e_of[i - 2], total_of[i - 2], z_of[(i - 2) // 2])
             if i < N_STEPS:
-                banks = logits_and_max(i, xt_of[i], 1)
-                exp_by_vector_and_scalar(banks[0:1], e_of[i])
-                total_of[i] = small.tile([P, A, J_STEP], F32, tag="total", name="total")
-                exp_by_scalar_alone(banks[1], e_of[i], total_of[i])
+                exponentials(logits_and_max(i, xt_of[i], 1), e_of[i], total_of[i])
             if 0 <= i - 1 < N_STEPS:
                 sum_of_units(e_of[i - 1], total_of[i - 1])
             if 0 <= i - 4 < N_STEPS:

@@ -27,8 +27,11 @@ ROW_TILES = B // P
 J_STEP = J_PASS // 2
 J_QUARTER = 4
 J_BANK = 2
-J_VECTOR = 5
+BANKS = J_STEP // J_BANK
 N_STEPS = ROW_TILES * J // J_STEP
+J_SCALAR = (3, 4, 4, 4)
+A_VECTOR = 2
+A_PIECE = 2
 
 FLOPS = 2 * J * B * F * A * U + 2 * A * B * J * U * F
 
@@ -52,8 +55,8 @@ def tile_iterativefeatureexclusion_pa_kernel(tc, xm, kernels, out):
         k_sb = [keep.tile([P, A, J_PASS, U], BF16, name="k_sb%d" % c) for c in range(N_PASS)]
         w_codes = [keep.tile([P, A * F], U32, name="w_codes%d" % c, align_bytes=64) for c in range(N_PASS)]
         w_scales = [keep.tile([P, A * F], U8, name="w_scales%d" % c, align_bytes=64) for c in range(N_PASS)]
-        z_codes = [keep.tile([P, A * P], U32, name="z_codes%d" % c, align_bytes=64) for c in range(N_PASS)]
-        z_scales = [keep.tile([P, A * P], U8, name="z_scales%d" % c, align_bytes=64) for c in range(N_PASS)]
+        z_codes = {}
+        z_scales = {}
 
         def place(step):
             return step // (2 * N_PASS), (step // 2) % N_PASS, (step % 2) * J_STEP
@@ -67,200 +70,269 @@ def tile_iterativefeatureexclusion_pa_kernel(tc, xm, kernels, out):
                         out=k_sb[c][:, a, jl0 : jl0 + J_STEP, :],
                         in_=kernels[j0 : j0 + J_STEP, a, :, :].rearrange("j f u -> f j u"),
                     )
-            x_sb = loads.tile([P, J_STEP, F], BF16)
+            x_sb = loads.tile([P, J_STEP, F], BF16, name="x_sb", bufs=4)
             nc.sync.dma_start(
                 out=x_sb[:], in_=xm[j0 : j0 + J_STEP, rt * P : (rt + 1) * P, :].rearrange("j b f -> b j f")
             )
             return x_sb
 
         def transpose_xm(x_sb):
-            xt_sb = loads.tile([P, J_STEP, P], BF16)
+            tiles = []
             for q in range(J_STEP // J_QUARTER):
-                js = slice(q * J_QUARTER, (q + 1) * J_QUARTER)
-                xt_ps = psum_tr.tile([P, J_QUARTER, P], BF16, tag="tr")
+                xt_ps = psum_tr.tile([P, J_QUARTER, P], BF16, tag="tr", name="xt_ps")
                 for i in range(J_QUARTER):
                     nc.tensor.transpose(xt_ps[:, i, :], x_sb[:, q * J_QUARTER + i, :], ident_bf[:])
-                nc.scalar.copy(out=xt_sb[:, js, :], in_=xt_ps[:])
-            return xt_sb
+                tiles.append(xt_ps)
+            return tiles
 
-        def logits_and_max(step, xt_sb, q):
+        def make_logits(step, xt_sb):
             rt, c, jl0 = place(step)
             banks = []
-            for half in range(J_QUARTER // J_BANK):
-                logits = psum_logits.tile([P, J_BANK, A, U], F32)
-                js0 = q * J_QUARTER + half * J_BANK
+            for k in range(BANKS):
+                logits = psum_logits.tile([P, J_BANK, A, U], F32, name="logits")
                 for i in range(J_BANK):
                     nc.tensor.matmul(
                         out=logits[:, i, :, :],
-                        lhsT=xt_sb[:, js0 + i, :],
-                        rhs=k_sb[c][:, :, jl0 + js0 + i, :],
+                        lhsT=xt_sb[:, k * J_BANK + i, :],
+                        rhs=k_sb[c][:, :, jl0 + k * J_BANK + i, :],
                         start=True,
                         stop=True,
                     )
-                shift = small.tile([P, J_BANK, A], F32)
-                nc.vector.tensor_reduce(out=shift[:], in_=logits[:], axis=AXIS.X, op=ALU.max, negate=True)
-                banks.append((logits, shift, js0))
+                banks.append(logits)
             return banks
 
-        def exponentials(banks, e_sb, total):
-            first = banks[0][2]
-            last = min(first + J_QUARTER, J_VECTOR)
-            for logits, shift, js0 in banks:
-                n = min(J_BANK, J_VECTOR - js0)
-                if n > 0:
-                    nc.vector.tensor_tensor(
-                        out=e_sb[:, :, js0 : js0 + n, :].rearrange("p a j u -> p j a u"),
-                        in0=logits[:, 0:n, :, :],
-                        in1=shift[:, 0:n, :].unsqueeze(3).to_broadcast([P, n, A, U]),
-                        op=ALU.add,
+        def exponentials(step, banks):
+            js = J_SCALAR[place(step)[0]]
+            e_sb = work.tile([P, A, J_STEP, U], F32, name="e_sb", bufs=4)
+            total = small.tile([P, A, J_STEP], F32, name="total")
+            shifts = []
+            for k in range(BANKS):
+                shift = small.tile([P, J_BANK, A], F32, name="shift%d" % k)
+                nc.vector.tensor_reduce(out=shift[:], in_=banks[k][:], axis=AXIS.X, op=ALU.max, negate=True)
+                shifts.append(shift)
+            for j in range(js):
+                k, i = j // J_BANK, j % J_BANK
+                for a in range(A):
+                    nc.scalar.activation(
+                        out=e_sb[:, a, j, :],
+                        in_=banks[k][:, i, a, :],
+                        func=ACT.Exp,
+                        bias=shifts[k][:, i, a : a + 1],
+                        accum_out=total[:, a, j : j + 1],
                     )
-            if last > first:
-                done = e_sb[:, :, first:last, :]
-                nc.scalar.activation(out=done, in_=done, func=ACT.Exp)
-            for logits, shift, js0 in banks:
-                for i in range(J_BANK):
-                    if js0 + i >= J_VECTOR:
-                        for a in range(A):
-                            nc.scalar.activation(
-                                out=e_sb[:, a, js0 + i, :],
-                                in_=logits[:, i, a, :],
-                                func=ACT.Exp,
-                                bias=shift[:, i, a : a + 1],
-                                accum_out=total[:, a, js0 + i : js0 + i + 1],
-                            )
+            for k in range(js // J_BANK, BANKS):
+                lo = max(js, k * J_BANK)
+                hi = (k + 1) * J_BANK
+                i0 = lo - k * J_BANK
+                nc.vector.tensor_tensor(
+                    out=e_sb[:, :, lo:hi, :].rearrange("p a j u -> p j a u"),
+                    in0=banks[k][:, i0:J_BANK, :, :],
+                    in1=shifts[k][:, i0:J_BANK, :].unsqueeze(3).to_broadcast([P, hi - lo, A, U]),
+                    op=ALU.add,
+                )
+            done = e_sb[:, :, js:J_STEP, :]
+            nc.scalar.activation(out=done, in_=done, func=ACT.Exp)
+            return e_sb, total
 
-        def sum_of_units(e_sb, total):
+        def sum_of_units(step, e_sb, total):
+            js = J_SCALAR[place(step)[0]]
             nc.vector.tensor_reduce(
-                out=total[:, :, 0:J_VECTOR], in_=e_sb[:, :, 0:J_VECTOR, :], axis=AXIS.X, op=ALU.add
+                out=total[:, :, js:J_STEP], in_=e_sb[:, :, js:J_STEP, :], axis=AXIS.X, op=ALU.add
             )
 
-        def normalise(step, e_sb, total, z_sb):
-            rt, c, jl0 = place(step)
-            inverse = small.tile([P, A, J_STEP], F32)
-            nc.vector.reciprocal(out=inverse[:], in_=total[:])
-            nc.gpsimd.tensor_tensor(
-                out=z_sb[:, :, jl0 : jl0 + J_STEP, :],
-                in0=e_sb[:],
-                in1=inverse[:].unsqueeze(3).to_broadcast([P, A, J_STEP, U]),
+        def invert(total, inverse, heads):
+            nc.vector.reciprocal(out=inverse[:, heads, :], in_=total[:, heads, :])
+
+        def normalise(engine, step, e_sb, inverse, z_sb, heads):
+            jl0 = place(step)[2]
+            n = heads.stop - heads.start
+            engine.tensor_tensor(
+                out=z_sb[:, heads, jl0 : jl0 + J_STEP, :],
+                in0=e_sb[:, heads, :, :],
+                in1=inverse[:, heads, :].unsqueeze(3).to_broadcast([P, n, J_STEP, U]),
                 op=ALU.mult,
             )
 
-        def transpose_z(z_sb, grouped, pair):
-            zt = psum_tr.tile([P, 2, H, P], F32, tag="tr")
+        def transpose_words(tile, pair):
+            ps = psum_tr.tile([P, 2, H, P], F32, tag="tr", name="ps")
             for ai in range(2):
-                words = z_sb[:, 2 * pair + ai, :, :].rearrange("p j u -> p (j u)").bitcast(F32)
+                words = tile[:, 2 * pair + ai, :, :].rearrange("p j u -> p (j u)").bitcast(F32)
                 for h in range(H):
                     nc.tensor.transpose(
-                        zt[:, ai, h, :], words.rearrange("p (w h) -> p w h", h=H)[:, :, h], ident_f32[:]
+                        ps[:, ai, h, :], words.rearrange("p (w h) -> p w h", h=H)[:, :, h], ident_f32[:]
                     )
+            return ps
+
+        def group_z(ps, grouped, pair):
             nc.scalar.copy(
                 out=grouped[:, 2 * pair : 2 * pair + 2, :, :].rearrange("p a b t -> p (a b t)").bitcast(F32),
-                in_=zt[:].rearrange("p a h b -> p a b h"),
+                in_=ps[:].rearrange("p a h b -> p a b h"),
             )
 
-        def quantise_weights(c):
-            grouped = work.tile([P, A, F, PACK], BF16, tag="grouped", align_bytes=64)
-            for pair in range(A // 2):
-                wt = psum_tr.tile([P, 2, 2, F], F32, tag="tr")
-                for ai in range(2):
-                    words = k_sb[c][:, 2 * pair + ai, :, :].rearrange("p j u -> p (j u)").bitcast(F32)
-                    for h in range(2):
-                        nc.tensor.transpose(
-                            wt[:, ai, h, :], words.rearrange("p (w h) -> p w h", h=2)[:, :, h], ident_f32[:]
-                        )
-                for ai in range(2):
-                    nc.scalar.activation(
-                        out=grouped[:, 2 * pair + ai, :, :].rearrange("p f (h e) -> p f h e", e=2),
-                        in_=wt[:, ai, :, :].bitcast(BF16).rearrange("p h (f e) -> p f h e", e=2),
-                        func=ACT.Exp,
-                        scale=2.0,
-                    )
+        def group_w(ps, grouped, pair):
+            for ai in range(2):
+                nc.scalar.activation(
+                    out=grouped[:, 2 * pair + ai, :, :].rearrange("p f (h e) -> p f h e", e=2),
+                    in_=ps[:, ai, :, :].bitcast(BF16).rearrange("p h (f e) -> p f h e", e=2),
+                    func=ACT.Exp,
+                    scale=2.0,
+                )
+
+        def quantise(codes, scales, grouped):
             nc.vector.quantize_mx(
-                out=w_codes[c][:].bitcast(FP8X4),
-                scales=w_scales[c][:],
-                in_=grouped[:].rearrange("p a f t -> p (a f t)"),
+                out=codes[:].bitcast(FP8X4), scales=scales[:], in_=grouped[:].rearrange("p a n t -> p (a n t)")
             )
 
-        def finish_rows(rt):
-            prob = work.tile([P, A, F], F32, tag="prob", bufs=1)
-            total = small.tile([P, A], F32, tag="score_total")
-            for half in range(2):
-                scores = psum_tr.tile([P, A // 2, F], F32, tag="tr")
-                for ai in range(A // 2):
-                    cols = slice((half * 4 + ai) * P, (half * 4 + ai + 1) * P)
-                    for c in range(N_PASS):
-                        nc.tensor.matmul_mx(
-                            out=scores[:, ai, :],
-                            lhsT=z_codes[c][:, cols].bitcast(FP8X4),
-                            lhsT_scale=z_scales[c][:, cols],
-                            rhs=w_codes[c][:, cols].bitcast(FP8X4),
-                            rhs_scale=w_scales[c][:, cols],
-                            start=(c == 0),
-                            stop=(c == N_PASS - 1),
-                        )
-                top = small.tile([P, A // 2], F32, tag="score_top")
-                nc.vector.tensor_reduce(out=top[:], in_=scores[:], axis=AXIS.X, op=ALU.max)
-                shift = small.tile([P, A // 2], F32, tag="score_shift")
-                nc.vector.tensor_scalar(out=shift[:], in0=top[:], scalar1=-1.0 / J, scalar2=None, op0=ALU.mult)
-                for ai in range(A // 2):
-                    a = half * 4 + ai
-                    nc.scalar.activation(
-                        out=prob[:, a, :],
-                        in_=scores[:, ai, :],
-                        func=ACT.Exp,
-                        bias=shift[:, ai : ai + 1],
-                        scale=1.0 / J,
-                        accum_out=total[:, a : a + 1],
+        def make_scores(piece, codes, scales):
+            scores = psum_tr.tile([P, A_PIECE, F], F32, tag="tr", name="scores")
+            for ai in range(A_PIECE):
+                cols = slice((piece * A_PIECE + ai) * P, (piece * A_PIECE + ai + 1) * P)
+                for c in range(N_PASS):
+                    nc.tensor.matmul_mx(
+                        out=scores[:, ai, :],
+                        lhsT=codes[c][:, cols].bitcast(FP8X4),
+                        lhsT_scale=scales[c][:, cols],
+                        rhs=w_codes[c][:, cols].bitcast(FP8X4),
+                        rhs_scale=w_scales[c][:, cols],
+                        start=(c == 0),
+                        stop=(c == N_PASS - 1),
                     )
-            inverse = small.tile([P, A], F32, tag="score_inverse")
+            return scores
+
+        def score_exponentials(scores):
+            prob = work.tile([P, A_PIECE, F], F32, name="prob", bufs=3)
+            total = small.tile([P, A_PIECE], F32, name="score_total")
+            top = small.tile([P, A_PIECE], F32, name="score_top")
+            nc.vector.tensor_reduce(out=top[:], in_=scores[:], axis=AXIS.X, op=ALU.max)
+            shift = small.tile([P, A_PIECE], F32, name="score_shift")
+            nc.vector.tensor_scalar(out=shift[:], in0=top[:], scalar1=-1.0 / J, scalar2=None, op0=ALU.mult)
+            for ai in range(A_PIECE):
+                nc.scalar.activation(
+                    out=prob[:, ai, :],
+                    in_=scores[:, ai, :],
+                    func=ACT.Exp,
+                    bias=shift[:, ai : ai + 1],
+                    scale=1.0 / J,
+                    accum_out=total[:, ai : ai + 1],
+                )
+            return prob, total
+
+        def finish_scores(rt, piece, prob, total):
+            inverse = small.tile([P, A_PIECE], F32, name="score_inverse")
             nc.vector.reciprocal(out=inverse[:], in_=total[:])
-            nc.gpsimd.tensor_tensor(
-                out=prob[:], in0=prob[:], in1=inverse[:].unsqueeze(2).to_broadcast([P, A, F]), op=ALU.mult
+            nc.vector.tensor_tensor(
+                out=prob[:], in0=prob[:], in1=inverse[:].unsqueeze(2).to_broadcast([P, A_PIECE, F]), op=ALU.mult
             )
-            nc.sync.dma_start(out=out[:, rt * P : (rt + 1) * P, :].rearrange("a b f -> b a f"), in_=prob[:])
+            nc.sync.dma_start(
+                out=out[piece * A_PIECE : (piece + 1) * A_PIECE, rt * P : (rt + 1) * P, :].rearrange("a b f -> b a f"),
+                in_=prob[:],
+            )
 
         x_of = {}
         xt_of = {}
+        logits_of = {}
         e_of = {}
         total_of = {}
         z_of = {}
-        grouped_of = {}
-        x_of[0] = load(0)
-        x_of[1] = load(1)
-        xt_of[0] = transpose_xm(x_of[0])
-        for i in range(N_STEPS + 4):
+        grouped = {}
+        pieces = []
+        made = []
+
+        def new_xt(step):
+            xt_of[step] = loads.tile([P, J_STEP, P], BF16, name="xt_sb", bufs=3)
+
+        for s in range(4):
+            x_of[s] = load(s)
+        for s in range(2):
+            new_xt(s)
+            for q, ps in enumerate(transpose_xm(x_of[s])):
+                nc.scalar.copy(out=xt_of[s][:, q * J_QUARTER : (q + 1) * J_QUARTER, :], in_=ps[:])
+        logits_of[0] = make_logits(0, xt_of[0])
+
+        ctx.enter_context(
+            tc.manual_schedule(
+                engines={
+                    mybir.EngineType.PE,
+                    mybir.EngineType.DVE,
+                    mybir.EngineType.Activation,
+                    mybir.EngineType.Pool,
+                }
+            )
+        )
+        n_made = 0
+        n_finished = 0
+        for i in range(N_STEPS + 4 + A // A_PIECE + 1):
+            s_z = i - 4
+            s_n = i - 1
+            if i + 4 < N_STEPS:
+                x_of[i + 4] = load(i + 4)
+
+            scores = None
+            if n_made < len(pieces):
+                rt, piece, codes, scales = pieces[n_made]
+                scores = make_scores(piece, codes, scales)
+            z_ps = []
+            w_ps = []
+            if 0 <= s_z < N_STEPS:
+                rt_z, c_z, jl_z = place(s_z)
+                first_pair = A // 4 * (s_z % 2)
+                if s_z % 2 == 0:
+                    grouped["z"] = work.tile([P, A, P, PACK], BF16, tag="grouped", name="grouped_z", align_bytes=64)
+                for pair in range(first_pair, first_pair + A // 4):
+                    z_ps.append((pair, transpose_words(z_of[s_z // 2], pair)))
+            xt_ps = []
             if i + 2 < N_STEPS:
-                x_of[i + 2] = load(i + 2)
+                new_xt(i + 2)
+                xt_ps = transpose_xm(x_of[i + 2])
+
+            if i < N_STEPS:
+                e_of[i], total_of[i] = exponentials(i, logits_of[i])
             if i + 1 < N_STEPS:
-                xt_of[i + 1] = transpose_xm(x_of[i + 1])
-            if i < N_STEPS:
-                e_of[i] = work.tile([P, A, J_STEP, U], F32, tag="e_sb", name="e_sb", bufs=4)
-                total_of[i] = small.tile([P, A, J_STEP], F32, tag="total", name="total")
-                exponentials(logits_and_max(i, xt_of[i], 0), e_of[i], total_of[i])
-            if 0 <= i - 2 < N_STEPS:
-                if (i - 2) % 2 == 0:
-                    z_of[(i - 2) // 2] = work.tile([P, A, J_PASS, U], BF16, tag="z_sb", name="z_sb")
-                normalise(i - 2, e_of[i - 2], total_of[i - 2], z_of[(i - 2) // 2])
-            if i < N_STEPS:
-                exponentials(logits_and_max(i, xt_of[i], 1), e_of[i], total_of[i])
-            if 0 <= i - 1 < N_STEPS:
-                sum_of_units(e_of[i - 1], total_of[i - 1])
-            if 0 <= i - 4 < N_STEPS:
-                unit = (i - 4) // 2
-                rt, c, jl0 = place(i - 4)
-                if (i - 4) % 2 == 0:
-                    grouped_of[unit] = work.tile([P, A, P, PACK], BF16, tag="grouped", name="grouped", align_bytes=64)
-                    transpose_z(z_of[unit], grouped_of[unit], 0)
-                    transpose_z(z_of[unit], grouped_of[unit], 1)
-                else:
-                    transpose_z(z_of[unit], grouped_of[unit], 2)
-                    transpose_z(z_of[unit], grouped_of[unit], 3)
-                    nc.vector.quantize_mx(
-                        out=z_codes[c][:].bitcast(FP8X4),
-                        scales=z_scales[c][:],
-                        in_=grouped_of[unit][:].rearrange("p a b t -> p (a b t)"),
-                    )
-                    if rt == 0:
-                        quantise_weights(c)
-                    if c == N_PASS - 1:
-                        finish_rows(rt)
+                logits_of[i + 1] = make_logits(i + 1, xt_of[i + 1])
+
+            for pair, ps in z_ps:
+                group_z(ps, grouped["z"], pair)
+            if xt_ps:
+                nc.scalar.copy(out=xt_of[i + 2][:, 0:J_QUARTER, :], in_=xt_ps[0][:])
+
+            if 0 <= s_n < N_STEPS:
+                sum_of_units(s_n, e_of[s_n], total_of[s_n])
+            if xt_ps:
+                nc.vector.tensor_copy(out=xt_of[i + 2][:, J_QUARTER:J_STEP, :], in_=xt_ps[1][:])
+            if 0 <= s_n < N_STEPS:
+                inverse = small.tile([P, A, J_STEP], F32, name="inverse")
+                invert(total_of[s_n], inverse, slice(0, A_VECTOR))
+            finishable = len(made)
+            if scores is not None:
+                made.append((rt, piece) + score_exponentials(scores))
+                n_made += 1
+            if 0 <= s_z < N_STEPS and s_z % 2 == 1:
+                z_codes[c_z] = work.tile(
+                    [P, A * P], U32, name="z_codes%d" % c_z, bufs=2 if c_z == 0 else 1, align_bytes=64
+                )
+                z_scales[c_z] = work.tile(
+                    [P, A * P], U8, name="z_scales%d" % c_z, bufs=2 if c_z == 0 else 1, align_bytes=64
+                )
+                quantise(z_codes[c_z], z_scales[c_z], grouped["z"])
+                if c_z == N_PASS - 1:
+                    for piece in range(A // A_PIECE):
+                        pieces.append(
+                            (rt_z, piece, [z_codes[c] for c in range(N_PASS)], [z_scales[c] for c in range(N_PASS)])
+                        )
+            if n_finished < finishable:
+                finish_scores(*made[n_finished])
+                n_finished += 1
+            if 0 <= s_n < N_STEPS:
+                if s_n % 2 == 0:
+                    z_of[s_n // 2] = work.tile([P, A, J_PASS, U], BF16, name="z_sb")
+                normalise(nc.vector, s_n, e_of[s_n], inverse, z_of[s_n // 2], slice(0, A_VECTOR))
+                invert(total_of[s_n], inverse, slice(A_VECTOR, A))
+                normalise(nc.gpsimd, s_n, e_of[s_n], inverse, z_of[s_n // 2], slice(A_VECTOR, A))
+
+            if 0 <= s_z < N_STEPS and rt_z == 0:
+                if s_z % 2 == 0:
+                    grouped["w"] = work.tile([P, A, F, PACK], BF16, tag="grouped", name="grouped_w", align_bytes=64)
+                for pair in range(first_pair, first_pair + A // 4):
+                    group_w(transpose_words(k_sb[c_z], pair), grouped["w"], pair)
+                if s_z % 2 == 1:
+                    quantise(w_codes[c_z], w_scales[c_z], grouped["w"])

@@ -29,8 +29,9 @@ J_QUARTER = 4
 J_BANK = 2
 BANKS = J_STEP // J_BANK
 N_STEPS = ROW_TILES * J // J_STEP
-J_SCALAR = (3, 4, 4, 4)
-A_VECTOR = 2
+J_SCALAR = (4, 6, 6, 6)
+XM_VECTOR = (0, 1, 1, 1)
+A_VECTOR = 1
 A_PIECE = 2
 
 FLOPS = 2 * J * B * F * A * U + 2 * A * B * J * U * F
@@ -64,16 +65,18 @@ def tile_iterativefeatureexclusion_pa_kernel(tc, xm, kernels, out):
         def load(step):
             rt, c, jl0 = place(step)
             j0 = c * J_PASS + jl0
-            if rt == 0:
-                for a in range(A):
-                    nc.sync.dma_start(
-                        out=k_sb[c][:, a, jl0 : jl0 + J_STEP, :],
-                        in_=kernels[j0 : j0 + J_STEP, a, :, :].rearrange("j f u -> f j u"),
-                    )
             x_sb = loads.tile([P, J_STEP, F], BF16, name="x_sb", bufs=4)
             nc.sync.dma_start(
                 out=x_sb[:], in_=xm[j0 : j0 + J_STEP, rt * P : (rt + 1) * P, :].rearrange("j b f -> b j f")
             )
+            if rt == 0:
+                n = J_BANK if step == 0 else J_STEP
+                for jl in range(0, J_STEP, n):
+                    for a in range(A):
+                        nc.sync.dma_start(
+                            out=k_sb[c][:, a, jl0 + jl : jl0 + jl + n, :],
+                            in_=kernels[j0 + jl : j0 + jl + n, a, :, :].rearrange("j f u -> f j u"),
+                        )
             return x_sb
 
         def transpose_xm(x_sb):
@@ -101,55 +104,59 @@ def tile_iterativefeatureexclusion_pa_kernel(tc, xm, kernels, out):
                 banks.append(logits)
             return banks
 
-        def exponentials(step, banks):
-            js = J_SCALAR[place(step)[0]]
-            e_sb = work.tile([P, A, J_STEP, U], F32, name="e_sb", bufs=4)
-            total = small.tile([P, A, J_STEP], F32, name="total")
+        def maxima(banks):
             shifts = []
             for k in range(BANKS):
                 shift = small.tile([P, J_BANK, A], F32, name="shift%d" % k)
                 nc.vector.tensor_reduce(out=shift[:], in_=banks[k][:], axis=AXIS.X, op=ALU.max, negate=True)
                 shifts.append(shift)
-            for j in range(js):
+            return shifts
+
+        def exponentials_by_scalar(step, banks, shifts):
+            e_sb = work.tile([P, J_STEP, A, U], F32, name="e_sb", bufs=3)
+            total = small.tile([P, J_STEP, A], F32, name="total")
+            for j in range(J_SCALAR[place(step)[0]]):
                 k, i = j // J_BANK, j % J_BANK
                 for a in range(A):
                     nc.scalar.activation(
-                        out=e_sb[:, a, j, :],
+                        out=e_sb[:, j, a, :],
                         in_=banks[k][:, i, a, :],
                         func=ACT.Exp,
                         bias=shifts[k][:, i, a : a + 1],
-                        accum_out=total[:, a, j : j + 1],
+                        accum_out=total[:, j, a : a + 1],
                     )
+            return e_sb, total
+
+        def exponentials_by_vector(step, banks, shifts, e_sb):
+            js = J_SCALAR[place(step)[0]]
             for k in range(js // J_BANK, BANKS):
-                lo = max(js, k * J_BANK)
-                hi = (k + 1) * J_BANK
-                i0 = lo - k * J_BANK
                 nc.vector.tensor_tensor(
-                    out=e_sb[:, :, lo:hi, :].rearrange("p a j u -> p j a u"),
-                    in0=banks[k][:, i0:J_BANK, :, :],
-                    in1=shifts[k][:, i0:J_BANK, :].unsqueeze(3).to_broadcast([P, hi - lo, A, U]),
+                    out=e_sb[:, k * J_BANK : (k + 1) * J_BANK, :, :],
+                    in0=banks[k][:],
+                    in1=shifts[k][:].unsqueeze(3).to_broadcast([P, J_BANK, A, U]),
                     op=ALU.add,
                 )
-            done = e_sb[:, :, js:J_STEP, :]
+            done = e_sb[:, js:J_STEP, :, :]
             nc.scalar.activation(out=done, in_=done, func=ACT.Exp)
-            return e_sb, total
 
         def sum_of_units(step, e_sb, total):
             js = J_SCALAR[place(step)[0]]
             nc.vector.tensor_reduce(
-                out=total[:, :, js:J_STEP], in_=e_sb[:, :, js:J_STEP, :], axis=AXIS.X, op=ALU.add
+                out=total[:, js:J_STEP, :], in_=e_sb[:, js:J_STEP, :, :], axis=AXIS.X, op=ALU.add
             )
 
-        def invert(total, inverse, heads):
-            nc.vector.reciprocal(out=inverse[:, heads, :], in_=total[:, heads, :])
+        def invert(total, heads, name):
+            inverse = small.tile([P, J_STEP, heads.stop - heads.start], F32, name=name)
+            nc.vector.reciprocal(out=inverse[:], in_=total[:, :, heads])
+            return inverse
 
         def normalise(engine, step, e_sb, inverse, z_sb, heads):
             jl0 = place(step)[2]
             n = heads.stop - heads.start
             engine.tensor_tensor(
                 out=z_sb[:, heads, jl0 : jl0 + J_STEP, :],
-                in0=e_sb[:, heads, :, :],
-                in1=inverse[:, heads, :].unsqueeze(3).to_broadcast([P, n, J_STEP, U]),
+                in0=e_sb[:, :, heads, :].rearrange("p j a u -> p a j u"),
+                in1=inverse[:].rearrange("p j a -> p a j").unsqueeze(3).to_broadcast([P, n, J_STEP, U]),
                 op=ALU.mult,
             )
 
@@ -159,12 +166,12 @@ def tile_iterativefeatureexclusion_pa_kernel(tc, xm, kernels, out):
                 words = tile[:, 2 * pair + ai, :, :].rearrange("p j u -> p (j u)").bitcast(F32)
                 for h in range(H):
                     nc.tensor.transpose(
-                        ps[:, ai, h, :], words.rearrange("p (w h) -> p w h", h=H)[:, :, h], ident_f32[:]
+                        ps[:, ai, h, :], words[:, h * P : (h + 1) * P], ident_f32[:]
                     )
             return ps
 
         def group_z(ps, grouped, pair):
-            nc.scalar.copy(
+            nc.vector.tensor_copy(
                 out=grouped[:, 2 * pair : 2 * pair + 2, :, :].rearrange("p a b t -> p (a b t)").bitcast(F32),
                 in_=ps[:].rearrange("p a h b -> p a b h"),
             )
@@ -199,11 +206,14 @@ def tile_iterativefeatureexclusion_pa_kernel(tc, xm, kernels, out):
                     )
             return scores
 
-        def score_exponentials(scores):
-            prob = work.tile([P, A_PIECE, F], F32, name="prob", bufs=3)
-            total = small.tile([P, A_PIECE], F32, name="score_total")
+        def score_maxima(scores):
             top = small.tile([P, A_PIECE], F32, name="score_top")
             nc.vector.tensor_reduce(out=top[:], in_=scores[:], axis=AXIS.X, op=ALU.max)
+            return top
+
+        def score_exponentials(scores, top):
+            prob = work.tile([P, A_PIECE, F], F32, name="prob", bufs=3)
+            total = small.tile([P, A_PIECE], F32, name="score_total")
             shift = small.tile([P, A_PIECE], F32, name="score_shift")
             nc.vector.tensor_scalar(out=shift[:], in0=top[:], scalar1=-1.0 / J, scalar2=None, op0=ALU.mult)
             for ai in range(A_PIECE):
@@ -217,9 +227,12 @@ def tile_iterativefeatureexclusion_pa_kernel(tc, xm, kernels, out):
                 )
             return prob, total
 
-        def finish_scores(rt, piece, prob, total):
+        def invert_score_total(total):
             inverse = small.tile([P, A_PIECE], F32, name="score_inverse")
             nc.vector.reciprocal(out=inverse[:], in_=total[:])
+            return inverse
+
+        def finish_scores(rt, piece, prob, inverse):
             nc.vector.tensor_tensor(
                 out=prob[:], in0=prob[:], in1=inverse[:].unsqueeze(2).to_broadcast([P, A_PIECE, F]), op=ALU.mult
             )
@@ -230,24 +243,31 @@ def tile_iterativefeatureexclusion_pa_kernel(tc, xm, kernels, out):
 
         x_of = {}
         xt_of = {}
+        xt_ps_of = {}
         logits_of = {}
+        shifts_of = {}
         e_of = {}
         total_of = {}
         z_of = {}
+        z_ps_of = {}
         grouped = {}
         pieces = []
-        made = []
+        scores_of = {}
+        made = {}
 
-        def new_xt(step):
+        def copy_xm(step):
             xt_of[step] = loads.tile([P, J_STEP, P], BF16, name="xt_sb", bufs=3)
+            for q in range(J_STEP // J_QUARTER):
+                copy = nc.vector.tensor_copy if q < XM_VECTOR[place(step)[0]] else nc.scalar.copy
+                copy(out=xt_of[step][:, q * J_QUARTER : (q + 1) * J_QUARTER, :], in_=xt_ps_of[step][q][:])
 
-        for s in range(4):
+        for s in range(5):
             x_of[s] = load(s)
         for s in range(2):
-            new_xt(s)
-            for q, ps in enumerate(transpose_xm(x_of[s])):
-                nc.scalar.copy(out=xt_of[s][:, q * J_QUARTER : (q + 1) * J_QUARTER, :], in_=ps[:])
+            xt_ps_of[s] = transpose_xm(x_of[s])
+            copy_xm(s)
         logits_of[0] = make_logits(0, xt_of[0])
+        xt_ps_of[2] = transpose_xm(x_of[2])
 
         ctx.enter_context(
             tc.manual_schedule(
@@ -259,80 +279,81 @@ def tile_iterativefeatureexclusion_pa_kernel(tc, xm, kernels, out):
                 }
             )
         )
+        shifts_of[0] = maxima(logits_of[0])
+        e_of[0], total_of[0] = exponentials_by_scalar(0, logits_of[0], shifts_of[0])
         n_made = 0
-        n_finished = 0
-        for i in range(N_STEPS + 4 + A // A_PIECE + 1):
-            s_z = i - 4
-            s_n = i - 1
-            if i + 4 < N_STEPS:
-                x_of[i + 4] = load(i + 4)
+        for i in range(N_STEPS + 6 + A // A_PIECE + 1):
+            if i + 5 < N_STEPS:
+                x_of[i + 5] = load(i + 5)
 
-            scores = None
-            if n_made < len(pieces):
-                rt, piece, codes, scales = pieces[n_made]
-                scores = make_scores(piece, codes, scales)
-            z_ps = []
-            w_ps = []
-            if 0 <= s_z < N_STEPS:
-                rt_z, c_z, jl_z = place(s_z)
-                first_pair = A // 4 * (s_z % 2)
-                if s_z % 2 == 0:
-                    grouped["z"] = work.tile([P, A, P, PACK], BF16, tag="grouped", name="grouped_z", align_bytes=64)
-                for pair in range(first_pair, first_pair + A // 4):
-                    z_ps.append((pair, transpose_words(z_of[s_z // 2], pair)))
-            xt_ps = []
-            if i + 2 < N_STEPS:
-                new_xt(i + 2)
-                xt_ps = transpose_xm(x_of[i + 2])
-
+            s = i - 1
+            if 0 <= s < N_STEPS:
+                sum_of_units(s, e_of[s], total_of[s])
+            if i - 1 in scores_of:
+                top = score_maxima(scores_of[i - 1][2])
             if i < N_STEPS:
-                e_of[i], total_of[i] = exponentials(i, logits_of[i])
+                exponentials_by_vector(i, logits_of[i], shifts_of[i], e_of[i])
+            if i - 1 in scores_of:
+                rt, piece, scores = scores_of[i - 1]
+                made[i] = (rt, piece) + score_exponentials(scores, top)
+            if i - 1 in made:
+                score_inverse = invert_score_total(made[i - 1][3])
+            if 0 <= s < N_STEPS:
+                inverse_v = invert(total_of[s], slice(0, A_VECTOR), "inverse_v")
+            s_q = i - 5
+            if 0 <= s_q < N_STEPS and s_q % 2 == 1:
+                rt, c, jl0 = place(s_q)
+                copies = 2 if c == 0 else 1
+                z_codes[c] = work.tile([P, A * P], U32, name="z_codes%d" % c, bufs=copies, align_bytes=64)
+                z_scales[c] = work.tile([P, A * P], U8, name="z_scales%d" % c, bufs=copies, align_bytes=64)
+                quantise(z_codes[c], z_scales[c], grouped[("z", s_q // 2)])
+                if c == N_PASS - 1:
+                    for piece in range(A // A_PIECE):
+                        pieces.append((rt, piece, [z_codes[d] for d in range(N_PASS)], [z_scales[d] for d in range(N_PASS)]))
+            if 0 <= s < N_STEPS:
+                if s % 2 == 0:
+                    z_of[s // 2] = work.tile([P, A, J_PASS, U], BF16, name="z_sb")
+                normalise(nc.vector, s, e_of[s], inverse_v, z_of[s // 2], slice(0, A_VECTOR))
+            if i - 1 in made:
+                rt, piece, prob, total = made[i - 1]
+                finish_scores(rt, piece, prob, score_inverse)
+            if 0 <= s < N_STEPS:
+                inverse_g = invert(total_of[s], slice(A_VECTOR, A), "inverse_g")
+                normalise(nc.gpsimd, s, e_of[s], inverse_g, z_of[s // 2], slice(A_VECTOR, A))
+
             if i + 1 < N_STEPS:
                 logits_of[i + 1] = make_logits(i + 1, xt_of[i + 1])
 
-            for pair, ps in z_ps:
-                group_z(ps, grouped["z"], pair)
-            if xt_ps:
-                nc.scalar.copy(out=xt_of[i + 2][:, 0:J_QUARTER, :], in_=xt_ps[0][:])
+            s = i - 4
+            if 0 <= s < N_STEPS:
+                if s % 2 == 0:
+                    grouped[("z", s // 2)] = work.tile([P, A, P, PACK], BF16, name="grouped_z", align_bytes=64)
+                for pair, ps in z_ps_of[s]:
+                    group_z(ps, grouped[("z", s // 2)], pair)
+            if i + 2 < N_STEPS:
+                copy_xm(i + 2)
+            if i + 1 < N_STEPS:
+                shifts_of[i + 1] = maxima(logits_of[i + 1])
+                e_of[i + 1], total_of[i + 1] = exponentials_by_scalar(i + 1, logits_of[i + 1], shifts_of[i + 1])
 
-            if 0 <= s_n < N_STEPS:
-                sum_of_units(s_n, e_of[s_n], total_of[s_n])
-            if xt_ps:
-                nc.vector.tensor_copy(out=xt_of[i + 2][:, J_QUARTER:J_STEP, :], in_=xt_ps[1][:])
-            if 0 <= s_n < N_STEPS:
-                inverse = small.tile([P, A, J_STEP], F32, name="inverse")
-                invert(total_of[s_n], inverse, slice(0, A_VECTOR))
-            finishable = len(made)
-            if scores is not None:
-                made.append((rt, piece) + score_exponentials(scores))
+            s_w = i - 4
+            if 0 <= s_w < N_STEPS and s_w % 2 == 1 and place(s_w)[0] == 0:
+                c = place(s_w)[1]
+                quantise(w_codes[c], w_scales[c], grouped[("w", s_w // 2)])
+
+            if n_made < len(pieces):
+                rt, piece, codes, scales = pieces[n_made]
+                scores_of[i] = (rt, piece, make_scores(piece, codes, scales))
                 n_made += 1
-            if 0 <= s_z < N_STEPS and s_z % 2 == 1:
-                z_codes[c_z] = work.tile(
-                    [P, A * P], U32, name="z_codes%d" % c_z, bufs=2 if c_z == 0 else 1, align_bytes=64
-                )
-                z_scales[c_z] = work.tile(
-                    [P, A * P], U8, name="z_scales%d" % c_z, bufs=2 if c_z == 0 else 1, align_bytes=64
-                )
-                quantise(z_codes[c_z], z_scales[c_z], grouped["z"])
-                if c_z == N_PASS - 1:
-                    for piece in range(A // A_PIECE):
-                        pieces.append(
-                            (rt_z, piece, [z_codes[c] for c in range(N_PASS)], [z_scales[c] for c in range(N_PASS)])
-                        )
-            if n_finished < finishable:
-                finish_scores(*made[n_finished])
-                n_finished += 1
-            if 0 <= s_n < N_STEPS:
-                if s_n % 2 == 0:
-                    z_of[s_n // 2] = work.tile([P, A, J_PASS, U], BF16, name="z_sb")
-                normalise(nc.vector, s_n, e_of[s_n], inverse, z_of[s_n // 2], slice(0, A_VECTOR))
-                invert(total_of[s_n], inverse, slice(A_VECTOR, A))
-                normalise(nc.gpsimd, s_n, e_of[s_n], inverse, z_of[s_n // 2], slice(A_VECTOR, A))
-
-            if 0 <= s_z < N_STEPS and rt_z == 0:
-                if s_z % 2 == 0:
-                    grouped["w"] = work.tile([P, A, F, PACK], BF16, tag="grouped", name="grouped_w", align_bytes=64)
-                for pair in range(first_pair, first_pair + A // 4):
-                    group_w(transpose_words(k_sb[c_z], pair), grouped["w"], pair)
-                if s_z % 2 == 1:
-                    quantise(w_codes[c_z], w_scales[c_z], grouped["w"])
+            s = i - 3
+            if 0 <= s < N_STEPS:
+                rt, c, jl0 = place(s)
+                pairs = range(2 * (s % 2), 2 * (s % 2) + 2)
+                z_ps_of[s] = [(pair, transpose_words(z_of[s // 2], pair)) for pair in pairs]
+            if i + 3 < N_STEPS:
+                xt_ps_of[i + 3] = transpose_xm(x_of[i + 3])
+            if 0 <= s < N_STEPS and rt == 0:
+                if s % 2 == 0:
+                    grouped[("w", s // 2)] = work.tile([P, A, F, PACK], BF16, name="grouped_w", bufs=1, align_bytes=64)
+                for pair in pairs:
+                    group_w(transpose_words(k_sb[c], pair), grouped[("w", s // 2)], pair)

@@ -25,14 +25,17 @@ J_PASS = P // UH
 N_PASS = J // J_PASS
 ROW_TILES = B // P
 J_STEP = J_PASS // 2
-J_QUARTER = 4
 J_BANK = 2
 BANKS = J_STEP // J_BANK
 N_STEPS = ROW_TILES * J // J_STEP
-J_SCALAR = (4, 6, 6, 6)
-XM_VECTOR = (0, 1, 1, 1)
+W_STEPS = 19
+J_SCALAR_W, J_SCALAR_REST = 5, 7
 A_VECTOR = 1
+A_VECTOR_LAST = 4
+XM_VECTOR = (0, 1, 1, 1)
 A_PIECE = 2
+N_LATE = 2
+A_PIECE_LAST = 4
 
 FLOPS = 2 * J * B * F * A * U + 2 * A * B * J * U * F
 
@@ -62,6 +65,9 @@ def tile_iterativefeatureexclusion_pa_kernel(tc, xm, kernels, out):
         def place(step):
             return step // (2 * N_PASS), (step // 2) % N_PASS, (step % 2) * J_STEP
 
+        def j_scalar(step):
+            return J_SCALAR_W if step < W_STEPS else J_SCALAR_REST
+
         def load(step):
             rt, c, jl0 = place(step)
             j0 = c * J_PASS + jl0
@@ -80,13 +86,10 @@ def tile_iterativefeatureexclusion_pa_kernel(tc, xm, kernels, out):
             return x_sb
 
         def transpose_xm(x_sb):
-            tiles = []
-            for q in range(J_STEP // J_QUARTER):
-                xt_ps = psum_tr.tile([P, J_QUARTER, P], BF16, tag="tr", name="xt_ps")
-                for i in range(J_QUARTER):
-                    nc.tensor.transpose(xt_ps[:, i, :], x_sb[:, q * J_QUARTER + i, :], ident_bf[:])
-                tiles.append(xt_ps)
-            return tiles
+            xt_ps = psum_tr.tile([P, J_STEP, P], BF16, tag="tr", name="xt_ps")
+            for j in range(J_STEP):
+                nc.tensor.transpose(xt_ps[:, j, :], x_sb[:, j, :], ident_bf[:])
+            return xt_ps
 
         def make_logits(step, xt_sb):
             rt, c, jl0 = place(step)
@@ -115,32 +118,41 @@ def tile_iterativefeatureexclusion_pa_kernel(tc, xm, kernels, out):
         def exponentials_by_scalar(step, banks, shifts):
             e_sb = work.tile([P, J_STEP, A, U], F32, name="e_sb", bufs=3)
             total = small.tile([P, J_STEP, A], F32, name="total")
-            for j in range(J_SCALAR[place(step)[0]]):
-                k, i = j // J_BANK, j % J_BANK
-                for a in range(A):
-                    nc.scalar.activation(
-                        out=e_sb[:, j, a, :],
-                        in_=banks[k][:, i, a, :],
-                        func=ACT.Exp,
-                        bias=shifts[k][:, i, a : a + 1],
-                        accum_out=total[:, j, a : a + 1],
-                    )
+            js = j_scalar(step)
+            for j in range(js - js % J_BANK):
+                exponentials_of_j(j, banks, shifts, e_sb, total)
             return e_sb, total
 
-        def exponentials_by_vector(step, banks, shifts, e_sb):
-            js = J_SCALAR[place(step)[0]]
+        def exponentials_of_j(j, banks, shifts, e_sb, total):
+            k, i = j // J_BANK, j % J_BANK
+            for a in range(A):
+                nc.scalar.activation(
+                    out=e_sb[:, j, a, :],
+                    in_=banks[k][:, i, a, :],
+                    func=ACT.Exp,
+                    bias=shifts[k][:, i, a : a + 1],
+                    accum_out=total[:, j, a : a + 1],
+                )
+
+        def exponentials_by_vector(step, banks, shifts, e_sb, total):
+            js = j_scalar(step)
             for k in range(js // J_BANK, BANKS):
+                lo = max(js, k * J_BANK)
+                hi = (k + 1) * J_BANK
+                i0 = lo - k * J_BANK
                 nc.vector.tensor_tensor(
-                    out=e_sb[:, k * J_BANK : (k + 1) * J_BANK, :, :],
-                    in0=banks[k][:],
-                    in1=shifts[k][:].unsqueeze(3).to_broadcast([P, J_BANK, A, U]),
+                    out=e_sb[:, lo:hi, :, :],
+                    in0=banks[k][:, i0:J_BANK, :, :],
+                    in1=shifts[k][:, i0:J_BANK, :].unsqueeze(3).to_broadcast([P, hi - lo, A, U]),
                     op=ALU.add,
                 )
+            for j in range(js - js % J_BANK, js):
+                exponentials_of_j(j, banks, shifts, e_sb, total)
             done = e_sb[:, js:J_STEP, :, :]
             nc.scalar.activation(out=done, in_=done, func=ACT.Exp)
 
         def sum_of_units(step, e_sb, total):
-            js = J_SCALAR[place(step)[0]]
+            js = j_scalar(step)
             nc.vector.tensor_reduce(
                 out=total[:, js:J_STEP, :], in_=e_sb[:, js:J_STEP, :, :], axis=AXIS.X, op=ALU.add
             )
@@ -170,8 +182,8 @@ def tile_iterativefeatureexclusion_pa_kernel(tc, xm, kernels, out):
                     )
             return ps
 
-        def group_z(ps, grouped, pair):
-            nc.vector.tensor_copy(
+        def group_z(copy, ps, grouped, pair):
+            copy(
                 out=grouped[:, 2 * pair : 2 * pair + 2, :, :].rearrange("p a b t -> p (a b t)").bitcast(F32),
                 in_=ps[:].rearrange("p a h b -> p a b h"),
             )
@@ -185,38 +197,43 @@ def tile_iterativefeatureexclusion_pa_kernel(tc, xm, kernels, out):
                     scale=2.0,
                 )
 
-        def quantise(codes, scales, grouped):
+        def quantise(codes, scales, grouped, half):
+            heads = slice(half * A // 2, (half + 1) * A // 2)
+            cols = slice(half * A // 2 * P, (half + 1) * A // 2 * P)
             nc.vector.quantize_mx(
-                out=codes[:].bitcast(FP8X4), scales=scales[:], in_=grouped[:].rearrange("p a n t -> p (a n t)")
+                out=codes[:, cols].bitcast(FP8X4),
+                scales=scales[:, cols],
+                in_=grouped[:, heads, :, :].rearrange("p a n t -> p (a n t)"),
             )
 
-        def make_scores(piece, codes, scales):
-            scores = psum_tr.tile([P, A_PIECE, F], F32, tag="tr", name="scores")
-            for ai in range(A_PIECE):
-                cols = slice((piece * A_PIECE + ai) * P, (piece * A_PIECE + ai + 1) * P)
-                for c in range(N_PASS):
+        def make_scores(scores, heads, codes, scales, passes):
+            for ai, a in enumerate(heads):
+                cols = slice(a * P, (a + 1) * P)
+                for c in passes:
                     nc.tensor.matmul_mx(
                         out=scores[:, ai, :],
                         lhsT=codes[c][:, cols].bitcast(FP8X4),
                         lhsT_scale=scales[c][:, cols],
                         rhs=w_codes[c][:, cols].bitcast(FP8X4),
                         rhs_scale=w_scales[c][:, cols],
-                        start=(c == 0),
-                        stop=(c == N_PASS - 1),
+                        start=(c == passes[0]),
+                        stop=(c == passes[-1]),
                     )
-            return scores
 
-        def score_maxima(scores):
-            top = small.tile([P, A_PIECE], F32, name="score_top")
-            nc.vector.tensor_reduce(out=top[:], in_=scores[:], axis=AXIS.X, op=ALU.max)
+        def score_maxima(scores, n):
+            top = small.tile([P, n], F32, name="score_top%d" % n)
+            nc.vector.tensor_reduce(out=top[:], in_=scores, axis=AXIS.X, op=ALU.max)
             return top
 
-        def score_exponentials(scores, top):
-            prob = work.tile([P, A_PIECE, F], F32, name="prob", bufs=3)
-            total = small.tile([P, A_PIECE], F32, name="score_total")
-            shift = small.tile([P, A_PIECE], F32, name="score_shift")
+        def score_exponentials(scores, top, n):
+            if n == A_PIECE:
+                prob = work.tile([P, n, F], F32, name="prob")
+            else:
+                prob = work.tile([P, n, F], F32, name="e_sb", bufs=3)
+            total = small.tile([P, n], F32, name="score_total%d" % n)
+            shift = small.tile([P, n], F32, name="score_shift%d" % n)
             nc.vector.tensor_scalar(out=shift[:], in0=top[:], scalar1=-1.0 / J, scalar2=None, op0=ALU.mult)
-            for ai in range(A_PIECE):
+            for ai in range(n):
                 nc.scalar.activation(
                     out=prob[:, ai, :],
                     in_=scores[:, ai, :],
@@ -227,18 +244,17 @@ def tile_iterativefeatureexclusion_pa_kernel(tc, xm, kernels, out):
                 )
             return prob, total
 
-        def invert_score_total(total):
-            inverse = small.tile([P, A_PIECE], F32, name="score_inverse")
+        def invert_score_total(total, n):
+            inverse = small.tile([P, n], F32, name="score_inverse%d" % n)
             nc.vector.reciprocal(out=inverse[:], in_=total[:])
             return inverse
 
-        def finish_scores(rt, piece, prob, inverse):
+        def finish_scores(rt, heads, prob, inverse):
             nc.vector.tensor_tensor(
-                out=prob[:], in0=prob[:], in1=inverse[:].unsqueeze(2).to_broadcast([P, A_PIECE, F]), op=ALU.mult
+                out=prob[:], in0=prob[:], in1=inverse[:].unsqueeze(2).to_broadcast([P, len(heads), F]), op=ALU.mult
             )
             nc.sync.dma_start(
-                out=out[piece * A_PIECE : (piece + 1) * A_PIECE, rt * P : (rt + 1) * P, :].rearrange("a b f -> b a f"),
-                in_=prob[:],
+                out=out[heads[0] : heads[-1] + 1, rt * P : (rt + 1) * P, :].rearrange("a b f -> b a f"), in_=prob[:]
             )
 
         x_of = {}
@@ -256,10 +272,9 @@ def tile_iterativefeatureexclusion_pa_kernel(tc, xm, kernels, out):
         made = {}
 
         def copy_xm(step):
-            xt_of[step] = loads.tile([P, J_STEP, P], BF16, name="xt_sb", bufs=3)
-            for q in range(J_STEP // J_QUARTER):
-                copy = nc.vector.tensor_copy if q < XM_VECTOR[place(step)[0]] else nc.scalar.copy
-                copy(out=xt_of[step][:, q * J_QUARTER : (q + 1) * J_QUARTER, :], in_=xt_ps_of[step][q][:])
+            xt_of[step] = loads.tile([P, J_STEP, P], BF16, name="xt_sb", bufs=2)
+            copy = nc.vector.tensor_copy if XM_VECTOR[place(step)[0]] else nc.scalar.copy
+            copy(out=xt_of[step][:], in_=xt_ps_of[step][:])
 
         for s in range(5):
             x_of[s] = load(s)
@@ -282,7 +297,7 @@ def tile_iterativefeatureexclusion_pa_kernel(tc, xm, kernels, out):
         shifts_of[0] = maxima(logits_of[0])
         e_of[0], total_of[0] = exponentials_by_scalar(0, logits_of[0], shifts_of[0])
         n_made = 0
-        for i in range(N_STEPS + 6 + A // A_PIECE + 1):
+        for i in range(N_STEPS + 7):
             if i + 5 < N_STEPS:
                 x_of[i + 5] = load(i + 5)
 
@@ -290,36 +305,43 @@ def tile_iterativefeatureexclusion_pa_kernel(tc, xm, kernels, out):
             if 0 <= s < N_STEPS:
                 sum_of_units(s, e_of[s], total_of[s])
             if i - 1 in scores_of:
-                top = score_maxima(scores_of[i - 1][2])
-            if i < N_STEPS:
-                exponentials_by_vector(i, logits_of[i], shifts_of[i], e_of[i])
-            if i - 1 in scores_of:
-                rt, piece, scores = scores_of[i - 1]
-                made[i] = (rt, piece) + score_exponentials(scores, top)
-            if i - 1 in made:
-                score_inverse = invert_score_total(made[i - 1][3])
-            if 0 <= s < N_STEPS:
-                inverse_v = invert(total_of[s], slice(0, A_VECTOR), "inverse_v")
+                rt_s, heads_s, scores = scores_of[i - 1]
+                if rt_s == ROW_TILES - 1:
+                    early_half = early[:, heads_s[0] : heads_s[-1] + 1, :]
+                    nc.vector.tensor_tensor(out=early_half, in0=scores[:], in1=early_half, op=ALU.add)
+                    scores = early_half
+                else:
+                    scores = scores[:]
+                top = score_maxima(scores, len(heads_s))
             s_q = i - 5
-            if 0 <= s_q < N_STEPS and s_q % 2 == 1:
+            if 0 <= s_q < N_STEPS:
                 rt, c, jl0 = place(s_q)
-                copies = 2 if c == 0 else 1
-                z_codes[c] = work.tile([P, A * P], U32, name="z_codes%d" % c, bufs=copies, align_bytes=64)
-                z_scales[c] = work.tile([P, A * P], U8, name="z_scales%d" % c, bufs=copies, align_bytes=64)
-                quantise(z_codes[c], z_scales[c], grouped[("z", s_q // 2)])
-                if c == N_PASS - 1:
-                    for piece in range(A // A_PIECE):
-                        pieces.append((rt, piece, [z_codes[d] for d in range(N_PASS)], [z_scales[d] for d in range(N_PASS)]))
+                if s_q % 2 == 0:
+                    copies = 2 if c < 2 else 1
+                    z_codes[c] = work.tile([P, A * P], U32, name="z_codes%d" % c, bufs=copies, align_bytes=64)
+                    z_scales[c] = work.tile([P, A * P], U8, name="z_scales%d" % c, bufs=copies, align_bytes=64)
+                quantise(z_codes[c], z_scales[c], grouped[("z", s_q // 2)], s_q % 2)
+                if s_q % 2 == 1 and c == N_PASS - 1:
+                    for a in range(0, A, A_PIECE) if rt < ROW_TILES - 1 else ():
+                        pieces.append((rt, range(a, a + A_PIECE), dict(z_codes), dict(z_scales)))
+            if 0 <= s < N_STEPS:
+                av = A_VECTOR if s < N_STEPS - 1 else A_VECTOR_LAST
+                inverse_v = invert(total_of[s], slice(0, av), "inverse_v")
+            if i - 1 in made:
+                score_inverse = invert_score_total(made[i - 1][3], len(made[i - 1][1]))
+            if i < N_STEPS:
+                exponentials_by_vector(i, logits_of[i], shifts_of[i], e_of[i], total_of[i])
+            if i - 1 in scores_of:
+                made[i] = (rt_s, heads_s) + score_exponentials(scores, top, len(heads_s))
             if 0 <= s < N_STEPS:
                 if s % 2 == 0:
                     z_of[s // 2] = work.tile([P, A, J_PASS, U], BF16, name="z_sb")
-                normalise(nc.vector, s, e_of[s], inverse_v, z_of[s // 2], slice(0, A_VECTOR))
+                normalise(nc.vector, s, e_of[s], inverse_v, z_of[s // 2], slice(0, av))
             if i - 1 in made:
-                rt, piece, prob, total = made[i - 1]
-                finish_scores(rt, piece, prob, score_inverse)
+                finish_scores(made[i - 1][0], made[i - 1][1], made[i - 1][2], score_inverse)
             if 0 <= s < N_STEPS:
-                inverse_g = invert(total_of[s], slice(A_VECTOR, A), "inverse_g")
-                normalise(nc.gpsimd, s, e_of[s], inverse_g, z_of[s // 2], slice(A_VECTOR, A))
+                inverse_g = invert(total_of[s], slice(av, A), "inverse_g")
+                normalise(nc.gpsimd, s, e_of[s], inverse_g, z_of[s // 2], slice(av, A))
 
             if i + 1 < N_STEPS:
                 logits_of[i + 1] = make_logits(i + 1, xt_of[i + 1])
@@ -328,8 +350,9 @@ def tile_iterativefeatureexclusion_pa_kernel(tc, xm, kernels, out):
             if 0 <= s < N_STEPS:
                 if s % 2 == 0:
                     grouped[("z", s // 2)] = work.tile([P, A, P, PACK], BF16, name="grouped_z", align_bytes=64)
-                for pair, ps in z_ps_of[s]:
-                    group_z(ps, grouped[("z", s // 2)], pair)
+                for n, (pair, ps) in enumerate(z_ps_of[s]):
+                    copy = nc.scalar.copy if s >= N_STEPS - 2 and n % 2 == 1 else nc.vector.tensor_copy
+                    group_z(copy, ps, grouped[("z", s // 2)], pair)
             if i + 2 < N_STEPS:
                 copy_xm(i + 2)
             if i + 1 < N_STEPS:
@@ -337,14 +360,22 @@ def tile_iterativefeatureexclusion_pa_kernel(tc, xm, kernels, out):
                 e_of[i + 1], total_of[i + 1] = exponentials_by_scalar(i + 1, logits_of[i + 1], shifts_of[i + 1])
 
             s_w = i - 4
-            if 0 <= s_w < N_STEPS and s_w % 2 == 1 and place(s_w)[0] == 0:
+            if 0 <= s_w < N_STEPS and place(s_w)[0] == 0:
                 c = place(s_w)[1]
-                quantise(w_codes[c], w_scales[c], grouped[("w", s_w // 2)])
+                quantise(w_codes[c], w_scales[c], grouped[("w", s_w // 2)], s_w % 2)
 
             if n_made < len(pieces):
-                rt, piece, codes, scales = pieces[n_made]
-                scores_of[i] = (rt, piece, make_scores(piece, codes, scales))
+                rt, heads, codes, scales = pieces[n_made]
+                scores = psum_tr.tile([P, A_PIECE, F], F32, tag="tr", name="scores")
+                make_scores(scores, heads, codes, scales, range(N_PASS))
+                scores_of[i] = (rt, heads, scores)
                 n_made += 1
+            s = i - 5
+            if N_STEPS - 2 <= s < N_STEPS:
+                heads = range(A_PIECE_LAST * (s % 2), A_PIECE_LAST * (s % 2) + A_PIECE_LAST)
+                scores = psum_logits.tile([P, A_PIECE_LAST, F], F32, name="logits")
+                make_scores(scores, heads, z_codes, z_scales, range(N_PASS - N_LATE, N_PASS))
+                scores_of[i] = (ROW_TILES - 1, heads, scores)
             s = i - 3
             if 0 <= s < N_STEPS:
                 rt, c, jl0 = place(s)
@@ -357,3 +388,13 @@ def tile_iterativefeatureexclusion_pa_kernel(tc, xm, kernels, out):
                     grouped[("w", s // 2)] = work.tile([P, A, F, PACK], BF16, name="grouped_w", bufs=1, align_bytes=64)
                 for pair in pairs:
                     group_w(transpose_words(k_sb[c], pair), grouped[("w", s // 2)], pair)
+            if i == N_STEPS:
+                early = work.tile([P, A, F], F32, name="e_sb", bufs=3)
+                early_ps = []
+                for a in range(0, A, A_PIECE_LAST):
+                    scores = psum_logits.tile([P, A_PIECE_LAST, F], F32, name="logits")
+                    make_scores(scores, range(a, a + A_PIECE_LAST), z_codes, z_scales, range(N_PASS - N_LATE))
+                    early_ps.append((a, scores))
+            if i == N_STEPS + 2:
+                for a, scores in early_ps:
+                    nc.scalar.copy(out=early[:, a : a + A_PIECE_LAST, :], in_=scores[:])

@@ -28,11 +28,13 @@ J_STEP = J_PASS // 2
 J_BANK = 2
 BANKS = J_STEP // J_BANK
 N_STEPS = ROW_TILES * J // J_STEP
+N_SOFT = J_STEP * A
+N_BANK = J_BANK * A
 W_STEPS = 19
-J_SCALAR_W, J_SCALAR_REST = 5, 7
+N_SCALAR_W, N_SCALAR_REST = 40, 53
 A_VECTOR = 1
-A_VECTOR_LAST = 4
-XM_VECTOR = (0, 1, 1, 1)
+A_VECTOR_LAST = 5
+XM_VECTOR = (1, 1, 1, 1)
 A_PIECE = 2
 N_LATE = 2
 A_PIECE_LAST = 4
@@ -65,8 +67,8 @@ def tile_iterativefeatureexclusion_pa_kernel(tc, xm, kernels, out):
         def place(step):
             return step // (2 * N_PASS), (step // 2) % N_PASS, (step % 2) * J_STEP
 
-        def j_scalar(step):
-            return J_SCALAR_W if step < W_STEPS else J_SCALAR_REST
+        def n_scalar(step):
+            return N_SCALAR_W if step < W_STEPS else N_SCALAR_REST
 
         def load(step):
             rt, c, jl0 = place(step)
@@ -95,10 +97,10 @@ def tile_iterativefeatureexclusion_pa_kernel(tc, xm, kernels, out):
             rt, c, jl0 = place(step)
             banks = []
             for k in range(BANKS):
-                logits = psum_logits.tile([P, J_BANK, A, U], F32, name="logits")
+                logits = psum_logits.tile([P, N_BANK, U], F32, name="logits")
                 for i in range(J_BANK):
                     nc.tensor.matmul(
-                        out=logits[:, i, :, :],
+                        out=logits[:, i * A : (i + 1) * A, :],
                         lhsT=xt_sb[:, k * J_BANK + i, :],
                         rhs=k_sb[c][:, :, jl0 + k * J_BANK + i, :],
                         start=True,
@@ -110,56 +112,52 @@ def tile_iterativefeatureexclusion_pa_kernel(tc, xm, kernels, out):
         def maxima(banks):
             shifts = []
             for k in range(BANKS):
-                shift = small.tile([P, J_BANK, A], F32, name="shift%d" % k)
+                shift = small.tile([P, N_BANK], F32, name="shift%d" % k)
                 nc.vector.tensor_reduce(out=shift[:], in_=banks[k][:], axis=AXIS.X, op=ALU.max, negate=True)
                 shifts.append(shift)
             return shifts
 
         def exponentials_by_scalar(step, banks, shifts):
-            e_sb = work.tile([P, J_STEP, A, U], F32, name="e_sb", bufs=3)
-            total = small.tile([P, J_STEP, A], F32, name="total")
-            js = j_scalar(step)
-            for j in range(js - js % J_BANK):
-                exponentials_of_j(j, banks, shifts, e_sb, total)
+            e_sb = work.tile([P, N_SOFT, U], F32, name="e_sb", bufs=3)
+            total = small.tile([P, N_SOFT], F32, name="total")
+            n = n_scalar(step)
+            exponentials_of(range(n - n % N_BANK), banks, shifts, e_sb, total)
             return e_sb, total
 
-        def exponentials_of_j(j, banks, shifts, e_sb, total):
-            k, i = j // J_BANK, j % J_BANK
-            for a in range(A):
+        def exponentials_of(softmaxes, banks, shifts, e_sb, total):
+            for g in softmaxes:
+                k, i = g // N_BANK, g % N_BANK
                 nc.scalar.activation(
-                    out=e_sb[:, j, a, :],
-                    in_=banks[k][:, i, a, :],
+                    out=e_sb[:, g, :],
+                    in_=banks[k][:, i, :],
                     func=ACT.Exp,
-                    bias=shifts[k][:, i, a : a + 1],
-                    accum_out=total[:, j, a : a + 1],
+                    bias=shifts[k][:, i : i + 1],
+                    accum_out=total[:, g : g + 1],
                 )
 
         def exponentials_by_vector(step, banks, shifts, e_sb, total):
-            js = j_scalar(step)
-            for k in range(js // J_BANK, BANKS):
-                lo = max(js, k * J_BANK)
-                hi = (k + 1) * J_BANK
-                i0 = lo - k * J_BANK
+            n = n_scalar(step)
+            for k in range(n // N_BANK, BANKS):
+                lo = max(n, k * N_BANK)
+                hi = (k + 1) * N_BANK
+                i0 = lo - k * N_BANK
                 nc.vector.tensor_tensor(
-                    out=e_sb[:, lo:hi, :, :],
-                    in0=banks[k][:, i0:J_BANK, :, :],
-                    in1=shifts[k][:, i0:J_BANK, :].unsqueeze(3).to_broadcast([P, hi - lo, A, U]),
+                    out=e_sb[:, lo:hi, :],
+                    in0=banks[k][:, i0:N_BANK, :],
+                    in1=shifts[k][:, i0:N_BANK].unsqueeze(2).to_broadcast([P, hi - lo, U]),
                     op=ALU.add,
                 )
-            for j in range(js - js % J_BANK, js):
-                exponentials_of_j(j, banks, shifts, e_sb, total)
-            done = e_sb[:, js:J_STEP, :, :]
+            exponentials_of(range(n - n % N_BANK, n), banks, shifts, e_sb, total)
+            done = e_sb[:, n:N_SOFT, :]
             nc.scalar.activation(out=done, in_=done, func=ACT.Exp)
 
         def sum_of_units(step, e_sb, total):
-            js = j_scalar(step)
-            nc.vector.tensor_reduce(
-                out=total[:, js:J_STEP, :], in_=e_sb[:, js:J_STEP, :, :], axis=AXIS.X, op=ALU.add
-            )
+            n = n_scalar(step)
+            nc.vector.tensor_reduce(out=total[:, n:N_SOFT], in_=e_sb[:, n:N_SOFT, :], axis=AXIS.X, op=ALU.add)
 
         def invert(total, heads, name):
             inverse = small.tile([P, J_STEP, heads.stop - heads.start], F32, name=name)
-            nc.vector.reciprocal(out=inverse[:], in_=total[:, :, heads])
+            nc.vector.reciprocal(out=inverse[:], in_=total[:].rearrange("p (j a) -> p j a", a=A)[:, :, heads])
             return inverse
 
         def normalise(engine, step, e_sb, inverse, z_sb, heads):
@@ -167,7 +165,7 @@ def tile_iterativefeatureexclusion_pa_kernel(tc, xm, kernels, out):
             n = heads.stop - heads.start
             engine.tensor_tensor(
                 out=z_sb[:, heads, jl0 : jl0 + J_STEP, :],
-                in0=e_sb[:, :, heads, :].rearrange("p j a u -> p a j u"),
+                in0=e_sb[:].rearrange("p (j a) u -> p a j u", a=A)[:, heads, :, :],
                 in1=inverse[:].rearrange("p j a -> p a j").unsqueeze(3).to_broadcast([P, n, J_STEP, U]),
                 op=ALU.mult,
             )
@@ -278,11 +276,6 @@ def tile_iterativefeatureexclusion_pa_kernel(tc, xm, kernels, out):
 
         for s in range(5):
             x_of[s] = load(s)
-        for s in range(2):
-            xt_ps_of[s] = transpose_xm(x_of[s])
-            copy_xm(s)
-        logits_of[0] = make_logits(0, xt_of[0])
-        xt_ps_of[2] = transpose_xm(x_of[2])
 
         ctx.enter_context(
             tc.manual_schedule(
@@ -294,8 +287,14 @@ def tile_iterativefeatureexclusion_pa_kernel(tc, xm, kernels, out):
                 }
             )
         )
+        xt_ps_of[0] = transpose_xm(x_of[0])
+        copy_xm(0)
+        logits_of[0] = make_logits(0, xt_of[0])
         shifts_of[0] = maxima(logits_of[0])
         e_of[0], total_of[0] = exponentials_by_scalar(0, logits_of[0], shifts_of[0])
+        xt_ps_of[1] = transpose_xm(x_of[1])
+        copy_xm(1)
+        xt_ps_of[2] = transpose_xm(x_of[2])
         n_made = 0
         for i in range(N_STEPS + 7):
             if i + 5 < N_STEPS:

@@ -31,12 +31,12 @@ N_STEPS = ROW_TILES * J // J_STEP
 N_SOFT = J_STEP * A
 N_BANK = J_BANK * A
 W_STEPS = 19
-N_SCALAR_W, N_SCALAR_REST = 40, 53
+N_SCALAR_W, N_SCALAR_REST, N_SCALAR_LAST = 40, 53, 40
 A_VECTOR = 1
-A_VECTOR_LAST = 5
+A_VECTOR_LAST = 4
 XM_VECTOR = (1, 1, 1, 1)
 A_PIECE = 2
-N_LATE = 2
+N_EARLY = 5
 A_PIECE_LAST = 4
 
 FLOPS = 2 * J * B * F * A * U + 2 * A * B * J * U * F
@@ -68,6 +68,8 @@ def tile_iterativefeatureexclusion_pa_kernel(tc, xm, kernels, out):
             return step // (2 * N_PASS), (step // 2) % N_PASS, (step % 2) * J_STEP
 
         def n_scalar(step):
+            if step == N_STEPS - 1:
+                return N_SCALAR_LAST
             return N_SCALAR_W if step < W_STEPS else N_SCALAR_REST
 
         def load(step):
@@ -78,13 +80,10 @@ def tile_iterativefeatureexclusion_pa_kernel(tc, xm, kernels, out):
                 out=x_sb[:], in_=xm[j0 : j0 + J_STEP, rt * P : (rt + 1) * P, :].rearrange("j b f -> b j f")
             )
             if rt == 0:
-                n = J_BANK if step == 0 else J_STEP
-                for jl in range(0, J_STEP, n):
-                    for a in range(A):
-                        nc.sync.dma_start(
-                            out=k_sb[c][:, a, jl0 + jl : jl0 + jl + n, :],
-                            in_=kernels[j0 + jl : j0 + jl + n, a, :, :].rearrange("j f u -> f j u"),
-                        )
+                for jl in range(J_STEP):
+                    nc.sync.dma_start(
+                        out=k_sb[c][:, :, jl0 + jl, :], in_=kernels[j0 + jl, :, :, :].rearrange("a f u -> f a u")
+                    )
             return x_sb
 
         def transpose_xm(x_sb):
@@ -166,12 +165,12 @@ def tile_iterativefeatureexclusion_pa_kernel(tc, xm, kernels, out):
             engine.tensor_tensor(
                 out=z_sb[:, heads, jl0 : jl0 + J_STEP, :],
                 in0=e_sb[:].rearrange("p (j a) u -> p a j u", a=A)[:, heads, :, :],
-                in1=inverse[:].rearrange("p j a -> p a j").unsqueeze(3).to_broadcast([P, n, J_STEP, U]),
+                in1=inverse.rearrange("p j a -> p a j").unsqueeze(3).to_broadcast([P, n, J_STEP, U]),
                 op=ALU.mult,
             )
 
-        def transpose_words(tile, pair):
-            ps = psum_tr.tile([P, 2, H, P], F32, tag="tr", name="ps")
+        def transpose_words(tile, pair, pool=psum_tr, tag="tr"):
+            ps = pool.tile([P, 2, H, P], F32, tag=tag, name="ps")
             for ai in range(2):
                 words = tile[:, 2 * pair + ai, :, :].rearrange("p j u -> p (j u)").bitcast(F32)
                 for h in range(H):
@@ -223,11 +222,7 @@ def tile_iterativefeatureexclusion_pa_kernel(tc, xm, kernels, out):
             nc.vector.tensor_reduce(out=top[:], in_=scores, axis=AXIS.X, op=ALU.max)
             return top
 
-        def score_exponentials(scores, top, n):
-            if n == A_PIECE:
-                prob = work.tile([P, n, F], F32, name="prob")
-            else:
-                prob = work.tile([P, n, F], F32, name="e_sb", bufs=3)
+        def score_exponentials(scores, top, prob, n):
             total = small.tile([P, n], F32, name="score_total%d" % n)
             shift = small.tile([P, n], F32, name="score_shift%d" % n)
             nc.vector.tensor_scalar(out=shift[:], in0=top[:], scalar1=-1.0 / J, scalar2=None, op0=ALU.mult)
@@ -240,7 +235,7 @@ def tile_iterativefeatureexclusion_pa_kernel(tc, xm, kernels, out):
                     scale=1.0 / J,
                     accum_out=total[:, ai : ai + 1],
                 )
-            return prob, total
+            return total
 
         def invert_score_total(total, n):
             inverse = small.tile([P, n], F32, name="score_inverse%d" % n)
@@ -249,10 +244,10 @@ def tile_iterativefeatureexclusion_pa_kernel(tc, xm, kernels, out):
 
         def finish_scores(rt, heads, prob, inverse):
             nc.vector.tensor_tensor(
-                out=prob[:], in0=prob[:], in1=inverse[:].unsqueeze(2).to_broadcast([P, len(heads), F]), op=ALU.mult
+                out=prob, in0=prob, in1=inverse[:].unsqueeze(2).to_broadcast([P, len(heads), F]), op=ALU.mult
             )
             nc.sync.dma_start(
-                out=out[heads[0] : heads[-1] + 1, rt * P : (rt + 1) * P, :].rearrange("a b f -> b a f"), in_=prob[:]
+                out=out[heads[0] : heads[-1] + 1, rt * P : (rt + 1) * P, :].rearrange("a b f -> b a f"), in_=prob
             )
 
         x_of = {}
@@ -266,6 +261,7 @@ def tile_iterativefeatureexclusion_pa_kernel(tc, xm, kernels, out):
         z_ps_of = {}
         grouped = {}
         pieces = []
+        early_ps = {}
         scores_of = {}
         made = {}
 
@@ -295,73 +291,74 @@ def tile_iterativefeatureexclusion_pa_kernel(tc, xm, kernels, out):
         xt_ps_of[1] = transpose_xm(x_of[1])
         copy_xm(1)
         xt_ps_of[2] = transpose_xm(x_of[2])
+        def quantise_z(step):
+            rt, c, jl0 = place(step)
+            if step % 2 == 0:
+                copies = 2 if c < 2 else 1
+                z_codes[c] = work.tile([P, A * P], U32, name="z_codes%d" % c, bufs=copies, align_bytes=64)
+                z_scales[c] = work.tile([P, A * P], U8, name="z_scales%d" % c, bufs=copies, align_bytes=64)
+            quantise(z_codes[c], z_scales[c], grouped[("z", step // 2)], step % 2)
+
+        def transpose_z(step):
+            for_pairs = range(2 * (step % 2), 2 * (step % 2) + 2)
+            return [(pair, transpose_words(z_of[step // 2], pair)) for pair in for_pairs]
+
+        def copy_z(copy, step):
+            if step % 2 == 0:
+                grouped[("z", step // 2)] = work.tile([P, A, P, PACK], BF16, name="grouped_z", align_bytes=64)
+            for pair, ps in z_ps_of[step]:
+                group_z(copy, ps, grouped[("z", step // 2)], pair)
+
         n_made = 0
-        for i in range(N_STEPS + 7):
+        for i in range(N_STEPS):
             if i + 5 < N_STEPS:
                 x_of[i + 5] = load(i + 5)
 
             s = i - 1
-            if 0 <= s < N_STEPS:
+            if s >= 0:
                 sum_of_units(s, e_of[s], total_of[s])
             if i - 1 in scores_of:
-                rt_s, heads_s, scores = scores_of[i - 1]
-                if rt_s == ROW_TILES - 1:
-                    early_half = early[:, heads_s[0] : heads_s[-1] + 1, :]
-                    nc.vector.tensor_tensor(out=early_half, in0=scores[:], in1=early_half, op=ALU.add)
-                    scores = early_half
-                else:
-                    scores = scores[:]
-                top = score_maxima(scores, len(heads_s))
-            s_q = i - 5
-            if 0 <= s_q < N_STEPS:
-                rt, c, jl0 = place(s_q)
-                if s_q % 2 == 0:
-                    copies = 2 if c < 2 else 1
-                    z_codes[c] = work.tile([P, A * P], U32, name="z_codes%d" % c, bufs=copies, align_bytes=64)
-                    z_scales[c] = work.tile([P, A * P], U8, name="z_scales%d" % c, bufs=copies, align_bytes=64)
-                quantise(z_codes[c], z_scales[c], grouped[("z", s_q // 2)], s_q % 2)
-                if s_q % 2 == 1 and c == N_PASS - 1:
-                    for a in range(0, A, A_PIECE) if rt < ROW_TILES - 1 else ():
+                top = score_maxima(scores_of[i - 1][2][:], A_PIECE)
+            if i >= 5:
+                quantise_z(i - 5)
+                rt, c, jl0 = place(i - 5)
+                if (i - 5) % 2 == 1 and c == N_PASS - 1:
+                    for a in range(0, A, A_PIECE):
                         pieces.append((rt, range(a, a + A_PIECE), dict(z_codes), dict(z_scales)))
-            if 0 <= s < N_STEPS:
-                av = A_VECTOR if s < N_STEPS - 1 else A_VECTOR_LAST
+            if s >= 0:
+                av = A_VECTOR if s < N_STEPS - 2 else A_VECTOR_LAST
                 inverse_v = invert(total_of[s], slice(0, av), "inverse_v")
             if i - 1 in made:
-                score_inverse = invert_score_total(made[i - 1][3], len(made[i - 1][1]))
-            if i < N_STEPS:
-                exponentials_by_vector(i, logits_of[i], shifts_of[i], e_of[i], total_of[i])
+                score_inverse = invert_score_total(made[i - 1][3], A_PIECE)
+            exponentials_by_vector(i, logits_of[i], shifts_of[i], e_of[i], total_of[i])
             if i - 1 in scores_of:
-                made[i] = (rt_s, heads_s) + score_exponentials(scores, top, len(heads_s))
-            if 0 <= s < N_STEPS:
+                prob = work.tile([P, A_PIECE, F], F32, name="prob")
+                score_total = score_exponentials(scores_of[i - 1][2][:], top, prob[:], A_PIECE)
+                made[i] = scores_of[i - 1][:2] + (prob[:], score_total)
+            if s >= 0:
                 if s % 2 == 0:
                     z_of[s // 2] = work.tile([P, A, J_PASS, U], BF16, name="z_sb")
-                normalise(nc.vector, s, e_of[s], inverse_v, z_of[s // 2], slice(0, av))
+                normalise(nc.vector, s, e_of[s], inverse_v[:], z_of[s // 2], slice(0, av))
             if i - 1 in made:
                 finish_scores(made[i - 1][0], made[i - 1][1], made[i - 1][2], score_inverse)
-            if 0 <= s < N_STEPS:
+            if s >= 0:
                 inverse_g = invert(total_of[s], slice(av, A), "inverse_g")
-                normalise(nc.gpsimd, s, e_of[s], inverse_g, z_of[s // 2], slice(av, A))
+                normalise(nc.gpsimd, s, e_of[s], inverse_g[:], z_of[s // 2], slice(av, A))
 
             if i + 1 < N_STEPS:
                 logits_of[i + 1] = make_logits(i + 1, xt_of[i + 1])
 
-            s = i - 4
-            if 0 <= s < N_STEPS:
-                if s % 2 == 0:
-                    grouped[("z", s // 2)] = work.tile([P, A, P, PACK], BF16, name="grouped_z", align_bytes=64)
-                for n, (pair, ps) in enumerate(z_ps_of[s]):
-                    copy = nc.scalar.copy if s >= N_STEPS - 2 and n % 2 == 1 else nc.vector.tensor_copy
-                    group_z(copy, ps, grouped[("z", s // 2)], pair)
+            if i >= 4:
+                copy_z(nc.vector.tensor_copy, i - 4)
             if i + 2 < N_STEPS:
                 copy_xm(i + 2)
             if i + 1 < N_STEPS:
                 shifts_of[i + 1] = maxima(logits_of[i + 1])
                 e_of[i + 1], total_of[i + 1] = exponentials_by_scalar(i + 1, logits_of[i + 1], shifts_of[i + 1])
-
-            s_w = i - 4
-            if 0 <= s_w < N_STEPS and place(s_w)[0] == 0:
-                c = place(s_w)[1]
-                quantise(w_codes[c], w_scales[c], grouped[("w", s_w // 2)], s_w % 2)
+            s = i - 4
+            if s >= 0 and place(s)[0] == 0:
+                c = place(s)[1]
+                quantise(w_codes[c], w_scales[c], grouped[("w", s // 2)], s % 2)
 
             if n_made < len(pieces):
                 rt, heads, codes, scales = pieces[n_made]
@@ -369,31 +366,58 @@ def tile_iterativefeatureexclusion_pa_kernel(tc, xm, kernels, out):
                 make_scores(scores, heads, codes, scales, range(N_PASS))
                 scores_of[i] = (rt, heads, scores)
                 n_made += 1
-            s = i - 5
-            if N_STEPS - 2 <= s < N_STEPS:
-                heads = range(A_PIECE_LAST * (s % 2), A_PIECE_LAST * (s % 2) + A_PIECE_LAST)
-                scores = psum_logits.tile([P, A_PIECE_LAST, F], F32, name="logits")
-                make_scores(scores, heads, z_codes, z_scales, range(N_PASS - N_LATE, N_PASS))
-                scores_of[i] = (ROW_TILES - 1, heads, scores)
             s = i - 3
-            if 0 <= s < N_STEPS:
-                rt, c, jl0 = place(s)
-                pairs = range(2 * (s % 2), 2 * (s % 2) + 2)
-                z_ps_of[s] = [(pair, transpose_words(z_of[s // 2], pair)) for pair in pairs]
+            if s >= 0:
+                z_ps_of[s] = transpose_z(s)
             if i + 3 < N_STEPS:
                 xt_ps_of[i + 3] = transpose_xm(x_of[i + 3])
-            if 0 <= s < N_STEPS and rt == 0:
+            if s >= 0 and place(s)[0] == 0:
+                c = place(s)[1]
                 if s % 2 == 0:
                     grouped[("w", s // 2)] = work.tile([P, A, F, PACK], BF16, name="grouped_w", bufs=1, align_bytes=64)
-                for pair in pairs:
+                for pair in range(2 * (s % 2), 2 * (s % 2) + 2):
                     group_w(transpose_words(k_sb[c], pair), grouped[("w", s // 2)], pair)
-            if i == N_STEPS:
-                early = work.tile([P, A, F], F32, name="e_sb", bufs=3)
-                early_ps = []
-                for a in range(0, A, A_PIECE_LAST):
-                    scores = psum_logits.tile([P, A_PIECE_LAST, F], F32, name="logits")
-                    make_scores(scores, range(a, a + A_PIECE_LAST), z_codes, z_scales, range(N_PASS - N_LATE))
-                    early_ps.append((a, scores))
-            if i == N_STEPS + 2:
-                for a, scores in early_ps:
-                    nc.scalar.copy(out=early[:, a : a + A_PIECE_LAST, :], in_=scores[:])
+            if i >= N_STEPS - 2:
+                half = i % 2
+                early_ps[half] = psum_tr.tile([P, A_PIECE_LAST, F], F32, tag="tr", name="early_ps")
+                heads = range(half * A_PIECE_LAST, (half + 1) * A_PIECE_LAST)
+                make_scores(early_ps[half], heads, z_codes, z_scales, range(N_EARLY))
+
+        s = N_STEPS - 1
+        copy_z(nc.vector.tensor_copy, s - 3)
+        z_ps_of[s - 2] = transpose_z(s - 2)
+        quantise_z(s - 4)
+        early = work.tile([P, A, F], F32, name="e_sb", bufs=3)
+        for half in range(2):
+            nc.scalar.copy(out=early[:, half * A_PIECE_LAST : (half + 1) * A_PIECE_LAST, :], in_=early_ps[half][:])
+        copy_z(nc.scalar.copy, s - 2)
+        sum_of_units(s, e_of[s], total_of[s])
+        quantise_z(s - 3)
+        inverse_v = invert(total_of[s], slice(0, A), "inverse_last")
+        grouped[("z", s // 2)] = work.tile([P, A, P, PACK], BF16, name="grouped_z", align_bytes=64)
+        for pair in range(A // 2):
+            heads = slice(2 * pair, 2 * pair + 2)
+            normalise(nc.vector, s, e_of[s], inverse_v[:, :, heads], z_of[s // 2], heads)
+            ps = transpose_words(z_of[s // 2], pair, psum_logits, "logits")
+            group_z(nc.scalar.copy, ps, grouped[("z", s // 2)], pair)
+        quantise_z(s - 2)
+        for half in range(2):
+            quantise_z(s - 1 + half)
+            for a in range(half * A_PIECE_LAST, (half + 1) * A_PIECE_LAST, A_PIECE):
+                scores_of[a] = psum_tr.tile([P, A_PIECE, F], F32, tag="tr", name="scores")
+                make_scores(scores_of[a], range(a, a + A_PIECE), z_codes, z_scales, range(N_EARLY, N_PASS))
+        n_pieces = A // A_PIECE
+        for p in range(n_pieces + 3):
+            if p >= 3:
+                last_inverse = invert_score_total(made[p - 3][1], A_PIECE)
+            if p < n_pieces:
+                part = early[:, p * A_PIECE : (p + 1) * A_PIECE, :]
+                nc.vector.tensor_tensor(out=part, in0=scores_of[p * A_PIECE][:], in1=part, op=ALU.add)
+            if 1 <= p <= n_pieces:
+                part = early[:, (p - 1) * A_PIECE : p * A_PIECE, :]
+                top = score_maxima(part, A_PIECE)
+            if p >= 3:
+                heads = range((p - 3) * A_PIECE, (p - 2) * A_PIECE)
+                finish_scores(ROW_TILES - 1, heads, made[p - 3][0], last_inverse)
+            if 1 <= p <= n_pieces:
+                made[p - 1] = (part, score_exponentials(part, top, part, A_PIECE))

from contextlib import ExitStack

import concourse.mybir as mybir
from concourse.masks import make_identity

BF16 = mybir.dt.bfloat16
F32 = mybir.dt.float32
U32 = mybir.dt.uint32
U8 = mybir.dt.uint8
FP8X4 = mybir.dt.float8_e4m3fn_x4
ALU = mybir.AluOpType
ACT = mybir.ActivationFunctionType
AXIS = mybir.AxisListType

P = 128
J = 128
B = 512
F = 128
A = 8
U = 32
PACK = 4
UH = U // PACK
H = 2
J_PASS = P // UH
N_PASS = J // J_PASS
ROW_TILES = B // P
J_STEP = J_PASS // 2
J_BANK = 2
BANKS = J_STEP // J_BANK
N_STEPS = ROW_TILES * J // J_STEP
N_SOFT = J_STEP * A
N_BANK = J_BANK * A
W_STEPS = 19
N_SCALAR_W, N_SCALAR_REST, N_SCALAR_LAST = 40, 53, 40
A_VECTOR = 1
A_VECTOR_LAST = 4
XM_VECTOR = (1, 1, 1, 1)
A_PIECE = 2
N_EARLY = 5
A_PIECE_LAST = 4

FLOPS = 2 * J * B * F * A * U + 2 * A * B * J * U * F


def tile_iterativefeatureexclusion_pa_kernel(tc, xm, kernels, out):
    nc = tc.nc
    with ExitStack() as ctx:
        const = ctx.enter_context(tc.tile_pool(name="const", bufs=1))
        keep = ctx.enter_context(tc.tile_pool(name="keep", bufs=1))
        loads = ctx.enter_context(tc.tile_pool(name="loads", bufs=3))
        work = ctx.enter_context(tc.tile_pool(name="work", bufs=2))
        small = ctx.enter_context(tc.tile_pool(name="small", bufs=4))
        psum_logits = ctx.enter_context(tc.psum_pool(name="psum_logits", bufs=4))
        psum_tr = ctx.enter_context(tc.psum_pool(name="psum_tr", bufs=4))

        ident_bf = const.tile([P, P], BF16)
        make_identity(nc, ident_bf[:])
        ident_f32 = const.tile([P, P], F32)
        make_identity(nc, ident_f32[:])

        k_sb = [keep.tile([P, A, J_PASS, U], BF16, name="k_sb%d" % c) for c in range(N_PASS)]
        w_codes = [keep.tile([P, A * F], U32, name="w_codes%d" % c, align_bytes=64) for c in range(N_PASS)]
        w_scales = [keep.tile([P, A * F], U8, name="w_scales%d" % c, align_bytes=64) for c in range(N_PASS)]
        z_codes = {}
        z_scales = {}

        def place(step):
            return step // (2 * N_PASS), (step // 2) % N_PASS, (step % 2) * J_STEP

        def n_scalar(step):
            if step == N_STEPS - 1:
                return N_SCALAR_LAST
            return N_SCALAR_W if step < W_STEPS else N_SCALAR_REST

        def load(step):
            rt, c, jl0 = place(step)
            j0 = c * J_PASS + jl0
            x_sb = loads.tile([P, J_STEP, F], BF16, name="x_sb", bufs=4)
            nc.sync.dma_start(
                out=x_sb[:], in_=xm[j0 : j0 + J_STEP, rt * P : (rt + 1) * P, :].rearrange("j b f -> b j f")
            )
            if rt == 0:
                for jl in range(J_STEP):
                    nc.sync.dma_start(
                        out=k_sb[c][:, :, jl0 + jl, :], in_=kernels[j0 + jl, :, :, :].rearrange("a f u -> f a u")
                    )
            return x_sb

        def transpose_xm(x_sb):
            xt_ps = psum_tr.tile([P, J_STEP, P], BF16, tag="tr", name="xt_ps")
            for j in range(J_STEP):
                nc.tensor.transpose(xt_ps[:, j, :], x_sb[:, j, :], ident_bf[:])
            return xt_ps

        def make_logits(step, xt_sb):
            rt, c, jl0 = place(step)
            banks = []
            for k in range(BANKS):
                logits = psum_logits.tile([P, N_BANK, U], F32, name="logits")
                for i in range(J_BANK):
                    nc.tensor.matmul(
                        out=logits[:, i * A : (i + 1) * A, :],
                        lhsT=xt_sb[:, k * J_BANK + i, :],
                        rhs=k_sb[c][:, :, jl0 + k * J_BANK + i, :],
                        start=True,
                        stop=True,
                    )
                banks.append(logits)
            return banks

        def maxima(banks):
            shifts = []
            for k in range(BANKS):
                shift = small.tile([P, N_BANK], F32, name="shift%d" % k)
                nc.vector.tensor_reduce(out=shift[:], in_=banks[k][:], axis=AXIS.X, op=ALU.max, negate=True)
                shifts.append(shift)
            return shifts

        def exponentials_by_scalar(step, banks, shifts):
            e_sb = work.tile([P, N_SOFT, U], F32, name="e_sb", bufs=3)
            total = small.tile([P, N_SOFT], F32, name="total")
            n = n_scalar(step)
            exponentials_of(range(n - n % N_BANK), banks, shifts, e_sb, total)
            return e_sb, total

        def exponentials_of(softmaxes, banks, shifts, e_sb, total):
            for g in softmaxes:
                k, i = g // N_BANK, g % N_BANK
                nc.scalar.activation(
                    out=e_sb[:, g, :],
                    in_=banks[k][:, i, :],
                    func=ACT.Exp,
                    bias=shifts[k][:, i : i + 1],
                    accum_out=total[:, g : g + 1],
                )

        def exponentials_by_vector(step, banks, shifts, e_sb, total):
            n = n_scalar(step)
            for k in range(n // N_BANK, BANKS):
                lo = max(n, k * N_BANK)
                hi = (k + 1) * N_BANK
                i0 = lo - k * N_BANK
                nc.vector.tensor_tensor(
                    out=e_sb[:, lo:hi, :],
                    in0=banks[k][:, i0:N_BANK, :],
                    in1=shifts[k][:, i0:N_BANK].unsqueeze(2).to_broadcast([P, hi - lo, U]),
                    op=ALU.add,
                )
            exponentials_of(range(n - n % N_BANK, n), banks, shifts, e_sb, total)
            done = e_sb[:, n:N_SOFT, :]
            nc.scalar.activation(out=done, in_=done, func=ACT.Exp)

        def sum_of_units(step, e_sb, total):
            n = n_scalar(step)
            nc.vector.tensor_reduce(out=total[:, n:N_SOFT], in_=e_sb[:, n:N_SOFT, :], axis=AXIS.X, op=ALU.add)

        def invert(total, heads, name):
            inverse = small.tile([P, J_STEP, heads.stop - heads.start], F32, name=name)
            nc.vector.reciprocal(out=inverse[:], in_=total[:].rearrange("p (j a) -> p j a", a=A)[:, :, heads])
            return inverse

        def normalise(engine, step, e_sb, inverse, z_sb, heads):
            jl0 = place(step)[2]
            n = heads.stop - heads.start
            engine.tensor_tensor(
                out=z_sb[:, heads, jl0 : jl0 + J_STEP, :],
                in0=e_sb[:].rearrange("p (j a) u -> p a j u", a=A)[:, heads, :, :],
                in1=inverse.rearrange("p j a -> p a j").unsqueeze(3).to_broadcast([P, n, J_STEP, U]),
                op=ALU.mult,
            )

        def transpose_words(tile, pair, pool=psum_tr, tag="tr"):
            ps = pool.tile([P, 2, H, P], F32, tag=tag, name="ps")
            for ai in range(2):
                words = tile[:, 2 * pair + ai, :, :].rearrange("p j u -> p (j u)").bitcast(F32)
                for h in range(H):
                    nc.tensor.transpose(
                        ps[:, ai, h, :], words[:, h * P : (h + 1) * P], ident_f32[:]
                    )
            return ps

        def group_z(copy, ps, grouped, pair):
            copy(
                out=grouped[:, 2 * pair : 2 * pair + 2, :, :].rearrange("p a b t -> p (a b t)").bitcast(F32),
                in_=ps[:].rearrange("p a h b -> p a b h"),
            )

        def group_w(ps, grouped, pair):
            for ai in range(2):
                nc.scalar.activation(
                    out=grouped[:, 2 * pair + ai, :, :].rearrange("p f (h e) -> p f h e", e=2),
                    in_=ps[:, ai, :, :].bitcast(BF16).rearrange("p h (f e) -> p f h e", e=2),
                    func=ACT.Exp,
                    scale=2.0,
                )

        def quantise(codes, scales, grouped, half):
            heads = slice(half * A // 2, (half + 1) * A // 2)
            cols = slice(half * A // 2 * P, (half + 1) * A // 2 * P)
            nc.vector.quantize_mx(
                out=codes[:, cols].bitcast(FP8X4),
                scales=scales[:, cols],
                in_=grouped[:, heads, :, :].rearrange("p a n t -> p (a n t)"),
            )

        def make_scores(scores, heads, codes, scales, passes):
            for ai, a in enumerate(heads):
                cols = slice(a * P, (a + 1) * P)
                for c in passes:
                    nc.tensor.matmul_mx(
                        out=scores[:, ai, :],
                        lhsT=codes[c][:, cols].bitcast(FP8X4),
                        lhsT_scale=scales[c][:, cols],
                        rhs=w_codes[c][:, cols].bitcast(FP8X4),
                        rhs_scale=w_scales[c][:, cols],
                        start=(c == passes[0]),
                        stop=(c == passes[-1]),
                    )

        def score_maxima(scores, n):
            top = small.tile([P, n], F32, name="score_top%d" % n)
            nc.vector.tensor_reduce(out=top[:], in_=scores, axis=AXIS.X, op=ALU.max)
            return top

        def score_exponentials(scores, top, prob, n):
            total = small.tile([P, n], F32, name="score_total%d" % n)
            shift = small.tile([P, n], F32, name="score_shift%d" % n)
            nc.vector.tensor_scalar(out=shift[:], in0=top[:], scalar1=-1.0 / J, scalar2=None, op0=ALU.mult)
            for ai in range(n):
                nc.scalar.activation(
                    out=prob[:, ai, :],
                    in_=scores[:, ai, :],
                    func=ACT.Exp,
                    bias=shift[:, ai : ai + 1],
                    scale=1.0 / J,
                    accum_out=total[:, ai : ai + 1],
                )
            return total

        def invert_score_total(total, n):
            inverse = small.tile([P, n], F32, name="score_inverse%d" % n)
            nc.vector.reciprocal(out=inverse[:], in_=total[:])
            return inverse

        def finish_scores(rt, heads, prob, inverse):
            nc.vector.tensor_tensor(
                out=prob, in0=prob, in1=inverse[:].unsqueeze(2).to_broadcast([P, len(heads), F]), op=ALU.mult
            )
            nc.sync.dma_start(
                out=out[heads[0] : heads[-1] + 1, rt * P : (rt + 1) * P, :].rearrange("a b f -> b a f"), in_=prob
            )

        x_of = {}
        xt_of = {}
        xt_ps_of = {}
        logits_of = {}
        shifts_of = {}
        e_of = {}
        total_of = {}
        z_of = {}
        z_ps_of = {}
        grouped = {}
        pieces = []
        early_ps = {}
        scores_of = {}
        made = {}

        def copy_xm(step):
            xt_of[step] = loads.tile([P, J_STEP, P], BF16, name="xt_sb", bufs=2)
            copy = nc.vector.tensor_copy if XM_VECTOR[place(step)[0]] else nc.scalar.copy
            copy(out=xt_of[step][:], in_=xt_ps_of[step][:])

        for s in range(5):
            x_of[s] = load(s)

        ctx.enter_context(
            tc.manual_schedule(
                engines={
                    mybir.EngineType.PE,
                    mybir.EngineType.DVE,
                    mybir.EngineType.Activation,
                    mybir.EngineType.Pool,
                }
            )
        )
        xt_ps_of[0] = transpose_xm(x_of[0])
        copy_xm(0)
        logits_of[0] = make_logits(0, xt_of[0])
        shifts_of[0] = maxima(logits_of[0])
        e_of[0], total_of[0] = exponentials_by_scalar(0, logits_of[0], shifts_of[0])
        xt_ps_of[1] = transpose_xm(x_of[1])
        copy_xm(1)
        xt_ps_of[2] = transpose_xm(x_of[2])
        def quantise_z(step):
            rt, c, jl0 = place(step)
            if step % 2 == 0:
                copies = 2 if c < 2 else 1
                z_codes[c] = work.tile([P, A * P], U32, name="z_codes%d" % c, bufs=copies, align_bytes=64)
                z_scales[c] = work.tile([P, A * P], U8, name="z_scales%d" % c, bufs=copies, align_bytes=64)
            quantise(z_codes[c], z_scales[c], grouped[("z", step // 2)], step % 2)

        def transpose_z(step):
            for_pairs = range(2 * (step % 2), 2 * (step % 2) + 2)
            return [(pair, transpose_words(z_of[step // 2], pair)) for pair in for_pairs]

        def copy_z(copy, step):
            if step % 2 == 0:
                grouped[("z", step // 2)] = work.tile([P, A, P, PACK], BF16, name="grouped_z", align_bytes=64)
            for pair, ps in z_ps_of[step]:
                group_z(copy, ps, grouped[("z", step // 2)], pair)

        n_made = 0
        for i in range(N_STEPS):
            if i + 5 < N_STEPS:
                x_of[i + 5] = load(i + 5)

            s = i - 1
            if s >= 0:
                sum_of_units(s, e_of[s], total_of[s])
            if i - 1 in scores_of:
                top = score_maxima(scores_of[i - 1][2][:], A_PIECE)
            if i >= 5:
                quantise_z(i - 5)
                rt, c, jl0 = place(i - 5)
                if (i - 5) % 2 == 1 and c == N_PASS - 1:
                    for a in range(0, A, A_PIECE):
                        pieces.append((rt, range(a, a + A_PIECE), dict(z_codes), dict(z_scales)))
            if s >= 0:
                av = A_VECTOR if s < N_STEPS - 2 else A_VECTOR_LAST
                inverse_v = invert(total_of[s], slice(0, av), "inverse_v")
            if i - 1 in made:
                score_inverse = invert_score_total(made[i - 1][3], A_PIECE)
            exponentials_by_vector(i, logits_of[i], shifts_of[i], e_of[i], total_of[i])
            if i - 1 in scores_of:
                prob = work.tile([P, A_PIECE, F], F32, name="prob")
                score_total = score_exponentials(scores_of[i - 1][2][:], top, prob[:], A_PIECE)
                made[i] = scores_of[i - 1][:2] + (prob[:], score_total)
            if s >= 0:
                if s % 2 == 0:
                    z_of[s // 2] = work.tile([P, A, J_PASS, U], BF16, name="z_sb")
                normalise(nc.vector, s, e_of[s], inverse_v[:], z_of[s // 2], slice(0, av))
            if i - 1 in made:
                finish_scores(made[i - 1][0], made[i - 1][1], made[i - 1][2], score_inverse)
            if s >= 0:
                inverse_g = invert(total_of[s], slice(av, A), "inverse_g")
                normalise(nc.gpsimd, s, e_of[s], inverse_g[:], z_of[s // 2], slice(av, A))

            if i + 1 < N_STEPS:
                logits_of[i + 1] = make_logits(i + 1, xt_of[i + 1])

            if i >= 4:
                copy_z(nc.vector.tensor_copy, i - 4)
            if i + 2 < N_STEPS:
                copy_xm(i + 2)
            if i + 1 < N_STEPS:
                shifts_of[i + 1] = maxima(logits_of[i + 1])
                e_of[i + 1], total_of[i + 1] = exponentials_by_scalar(i + 1, logits_of[i + 1], shifts_of[i + 1])
            s = i - 4
            if s >= 0 and place(s)[0] == 0:
                c = place(s)[1]
                quantise(w_codes[c], w_scales[c], grouped[("w", s // 2)], s % 2)

            if n_made < len(pieces):
                rt, heads, codes, scales = pieces[n_made]
                scores = psum_tr.tile([P, A_PIECE, F], F32, tag="tr", name="scores")
                make_scores(scores, heads, codes, scales, range(N_PASS))
                scores_of[i] = (rt, heads, scores)
                n_made += 1
            s = i - 3
            if s >= 0:
                z_ps_of[s] = transpose_z(s)
            if i + 3 < N_STEPS:
                xt_ps_of[i + 3] = transpose_xm(x_of[i + 3])
            if s >= 0 and place(s)[0] == 0:
                c = place(s)[1]
                if s % 2 == 0:
                    grouped[("w", s // 2)] = work.tile([P, A, F, PACK], BF16, name="grouped_w", bufs=1, align_bytes=64)
                for pair in range(2 * (s % 2), 2 * (s % 2) + 2):
                    group_w(transpose_words(k_sb[c], pair), grouped[("w", s // 2)], pair)
            if i >= N_STEPS - 2:
                half = i % 2
                early_ps[half] = psum_tr.tile([P, A_PIECE_LAST, F], F32, tag="tr", name="early_ps")
                heads = range(half * A_PIECE_LAST, (half + 1) * A_PIECE_LAST)
                make_scores(early_ps[half], heads, z_codes, z_scales, range(N_EARLY))

        s = N_STEPS - 1
        copy_z(nc.vector.tensor_copy, s - 3)
        z_ps_of[s - 2] = transpose_z(s - 2)
        quantise_z(s - 4)
        early = work.tile([P, A, F], F32, name="e_sb", bufs=3)
        for half in range(2):
            nc.scalar.copy(out=early[:, half * A_PIECE_LAST : (half + 1) * A_PIECE_LAST, :], in_=early_ps[half][:])
        copy_z(nc.scalar.copy, s - 2)
        sum_of_units(s, e_of[s], total_of[s])
        quantise_z(s - 3)
        inverse_v = invert(total_of[s], slice(0, A), "inverse_last")
        grouped[("z", s // 2)] = work.tile([P, A, P, PACK], BF16, name="grouped_z", align_bytes=64)
        for pair in range(A // 2):
            heads = slice(2 * pair, 2 * pair + 2)
            normalise(nc.vector, s, e_of[s], inverse_v[:, :, heads], z_of[s // 2], heads)
            ps = transpose_words(z_of[s // 2], pair, psum_logits, "logits")
            group_z(nc.scalar.copy, ps, grouped[("z", s // 2)], pair)
        quantise_z(s - 2)
        for half in range(2):
            quantise_z(s - 1 + half)
            for a in range(half * A_PIECE_LAST, (half + 1) * A_PIECE_LAST, A_PIECE):
                scores_of[a] = psum_tr.tile([P, A_PIECE, F], F32, tag="tr", name="scores")
                make_scores(scores_of[a], range(a, a + A_PIECE), z_codes, z_scales, range(N_EARLY, N_PASS))
        n_pieces = A // A_PIECE
        for p in range(n_pieces + 3):
            if p >= 3:
                last_inverse = invert_score_total(made[p - 3][1], A_PIECE)
            if p < n_pieces:
                part = early[:, p * A_PIECE : (p + 1) * A_PIECE, :]
                nc.vector.tensor_tensor(out=part, in0=scores_of[p * A_PIECE][:], in1=part, op=ALU.add)
            if 1 <= p <= n_pieces:
                part = early[:, (p - 1) * A_PIECE : p * A_PIECE, :]
                top = score_maxima(part, A_PIECE)
            if p >= 3:
                heads = range((p - 3) * A_PIECE, (p - 2) * A_PIECE)
                finish_scores(ROW_TILES - 1, heads, made[p - 3][0], last_inverse)
            if 1 <= p <= n_pieces:
                made[p - 1] = (part, score_exponentials(part, top, part, A_PIECE))
